import numpy as np
import ml_dtypes

BF16 = ml_dtypes.bfloat16


def bf(x):
    return np.asarray(x, np.float32).astype(BF16)


def f32(x):
    return np.asarray(x, np.float32)


def f64(x):
    return np.asarray(x).astype(np.float64)


def striped(idx):
    return np.tile(idx.reshape(-1, 16).T, (8, 1))


B, T, C, H, DK, DK0, S, N = 2, 1024, 256, 2, 128, 32, 4096, 2048
SCALE = DK0 ** -0.5


def softmax0(a):
    e = np.exp(a - a.max(axis=0, keepdims=True))
    return e / e.sum(axis=0, keepdims=True)


def setup_inputs():
    return {
        "q": bf(np.random.standard_normal((C, N))),
        "k": bf(np.random.standard_normal((C, N))),
        "v": bf(np.random.standard_normal((C, N))),
        "adj": bf(np.random.random((B, T, T)) < 0.5),
        "adj1": bf(np.random.random((B, T, T)) < 0.5),
        "attn_bias": bf(np.random.random((B, H, T, T))),
        "edge_bias": bf(0.75 * np.random.standard_normal((B, H, T, T))),
        "wq": bf(np.random.standard_normal((C, C)) / np.sqrt(C)),
        "bq": f32(0.1 * np.random.standard_normal((C, 1))),
        "wk": bf(np.random.standard_normal((C, C)) / np.sqrt(C)),
        "bk": f32(0.1 * np.random.standard_normal((C, 1))),
        "wv": bf(2.0 * np.random.standard_normal((C, C)) / np.sqrt(C)),
        "bv": f32(0.1 * np.random.standard_normal((C, 1))),
        "wo": bf(1.5 * np.random.standard_normal((C, C)) / np.sqrt(C)),
        "bo": f32(0.1 * np.random.standard_normal((C, 1))),
        "base": f32(np.random.standard_normal((C, S))),
        "offs": striped(np.random.permutation(S)[:N]),
    }


def reference(q, k, v, adj, adj1, attn_bias, edge_bias, wq, bq, wk, bk, wv, bv, wo, bo, base, offs):
    idx = offs[:16].T.reshape(-1)
    qh = f64(wq).T @ f64(q) + f64(bq)
    kh = f64(wk).T @ f64(k) + f64(bk)
    vh = f64(wv).T @ f64(v) + f64(bv)
    att = np.zeros((C, N), np.float64)
    for b in range(B):
        cols = slice(b * T, (b + 1) * T)
        for h in range(H):
            rows = slice(h * DK, (h + 1) * DK)
            x = SCALE * (kh[rows, cols].T @ qh[rows, cols]) * f64(adj[b])
            plong = softmax0(x * f64(attn_bias[b, h]))
            ploc = softmax0(x * f64(edge_bias[b, h]) * f64(adj1[b]))
            att[rows, cols] = vh[rows, cols] @ ploc + vh[rows, cols] @ plong
    y = f64(wo).T @ att
    out = f64(base).copy()
    out[:, idx] = y + f64(bo)
    return out

@@ -1,0 +1,221 @@
+from contextlib import ExitStack
+
+import concourse.mybir as mybir
+from concourse.masks import make_identity
+
+BF16, F32, U16 = mybir.dt.bfloat16, mybir.dt.float32, mybir.dt.uint16
+ALU = mybir.AluOpType
+ACT = mybir.ActivationFunctionType
+
+P = 128
+B, T, C, H, DK, S, N = 2, 1024, 256, 2, 128, 4096, 2048
+SCALE = 32.0**-0.5
+CB = C // P
+KT = T // P
+IC = 512
+NCH = T // IC
+IB = IC // P
+
+FLOPS = 4 * 2 * C * C * N + 3 * B * H * 2 * DK * T * T
+
+
+def tile_multiheadattention_b_kernel(
+    tc, q, k, v, adj, adj1, attn_bias, edge_bias, wq, bq, wk, bk, wv, bv, wo, bo, base, offs, out
+):
+    nc = tc.nc
+    with ExitStack() as ctx:
+        held = ctx.enter_context(tc.tile_pool(name="held", bufs=1))
+        work = ctx.enter_context(tc.tile_pool(name="work", bufs=1))
+
+        offsets = held.tile([P, N // 16], U16, name="offsets")
+        nc.sync.dma_start(offsets[:], offs)
+
+        ident_f32 = held.tile([P, P], F32, name="ident_f32")
+        make_identity(nc, ident_f32[:])
+        ident_bf16 = held.tile([P, P], BF16, name="ident_bf16")
+        make_identity(nc, ident_bf16[:])
+        ones_f32 = held.tile([P, P], F32, name="ones_f32")
+        nc.vector.memset(ones_f32[:], 1.0)
+
+        weights = {}
+        for name, w_dram in (("wk", wk), ("wq", wq), ("wv", wv), ("wo", wo)):
+            weights[name] = held.tile([P, CB, C], BF16, name=name)
+            nc.sync.dma_start(weights[name][:], w_dram.rearrange("(e p) c -> p e c", p=P))
+
+        windows = [held.tile([P, S], F32, name=f"window{cb}") for cb in range(CB)]
+
+        qh = held.tile([P, H, N], BF16, name="qh")
+        kh = held.tile([P, H, N], BF16, name="kh")
+        vaug = held.tile([P, B * KT, H, DK + 1], BF16, name="vaug")
+        bias_cols = held.tile([P, 3 * CB], F32, name="bias_cols")
+        bv_all = held.tile([P, C], F32, name="bv_all")
+        nc.sync.dma_start(bv_all[:], bv.rearrange("c one -> (c one)").partition_broadcast(P))
+
+        with (
+            tc.tile_pool(name="stage", bufs=1) as stage,
+            tc.psum_pool(name="proj_psum", bufs=2) as proj_psum,
+        ):
+            bias_rows = stage.tile([1, 3 * C], F32, name="bias_rows")
+            for j, b_dram in enumerate((bq, bk, bo)):
+                nc.sync.dma_start(bias_rows[0:1, j * C : (j + 1) * C], b_dram.rearrange("c one -> one c"))
+            one = stage.tile([1, 1], F32, name="one")
+            nc.vector.memset(one[:], 1.0)
+            bias_ps = proj_psum.tile([P, 3 * CB], F32, name="bias_ps")
+            for j in range(3 * CB):
+                nc.tensor.matmul(
+                    bias_ps[:, j : j + 1], lhsT=bias_rows[0:1, j * P : (j + 1) * P], rhs=one[:], start=True, stop=True
+                )
+            nc.vector.tensor_copy(bias_cols[:], bias_ps[:])
+
+            staged = {}
+            for name, x_dram in (("k", k), ("q", q), ("v", v)):
+                staged[name] = stage.tile([P, CB, N], BF16, name=name + "_sb")
+                nc.sync.dma_start(staged[name][:], x_dram.rearrange("(e p) n -> p e n", p=P))
+
+            for dst, w_sb, x_sb, first_col in ((kh, weights["wk"], staged["k"], CB), (qh, weights["wq"], staged["q"], 0)):
+                for h in range(H):
+                    for n in range(N // IC):
+                        proj_ps = proj_psum.tile([P, IC], F32, name="proj_ps")
+                        for e in range(CB):
+                            nc.tensor.matmul(
+                                proj_ps[:],
+                                lhsT=w_sb[:, e, h * P : (h + 1) * P],
+                                rhs=x_sb[:, e, n * IC : (n + 1) * IC],
+                                start=(e == 0),
+                                stop=(e == CB - 1),
+                            )
+                        nc.scalar.activation(
+                            dst[:, h, n * IC : (n + 1) * IC],
+                            proj_ps[:],
+                            ACT.Identity,
+                            bias=bias_cols[:, first_col + h : first_col + h + 1],
+                        )
+
+            nc.vector.memset(vaug[:, :, :, DK : DK + 1], 1.0)
+            for tb in range(B * KT):
+                v_ps = proj_psum.tile([P, C], F32, name="v_ps")
+                for e in range(CB):
+                    nc.tensor.matmul(
+                        v_ps[:],
+                        lhsT=staged["v"][:, e, tb * P : (tb + 1) * P],
+                        rhs=weights["wv"][:, e, :],
+                        start=(e == 0),
+                        stop=(e == CB - 1),
+                    )
+                nc.vector.tensor_tensor(
+                    vaug[:, tb, :, 0:DK],
+                    v_ps[:].rearrange("p (h d) -> p h d", h=H),
+                    bv_all[:].rearrange("p (h d) -> p h d", h=H),
+                    ALU.add,
+                )
+
+        late = ctx.enter_context(tc.tile_pool(name="late", bufs=1))
+        psum = ctx.enter_context(tc.psum_pool(name="psum", bufs=1))
+        y_sb = [late.tile([P, N], F32, name=f"y_sb{cb}") for cb in range(CB)]
+        bo_wide = [late.tile([P, N], F32, name=f"bo_wide{cb}") for cb in range(CB)]
+        for cb in range(CB):
+            nc.scalar.activation(
+                bo_wide[cb][:], bias_cols[:, 2 * CB + cb : 2 * CB + cb + 1].to_broadcast([P, N]), ACT.Copy
+            )
+
+        for b in range(B):
+            for ch in range(NCH):
+                lo = ch * IC
+                adj_sb = work.tile([P, KT, IC], BF16, name="adj_sb")
+                nc.sync.dma_start(adj_sb[:], adj[b, :, lo : lo + IC].rearrange("(k p) i -> p k i", p=P))
+                both_sb = work.tile([P, KT, IC], BF16, name="both_sb")
+                nc.sync.dma_start(both_sb[:], adj1[b, :, lo : lo + IC].rearrange("(k p) i -> p k i", p=P))
+                nc.vector.tensor_tensor(both_sb[:], both_sb[:], adj_sb[:], ALU.mult)
+
+                att_t = work.tile([P, IB, C], BF16, name="att_t", bufs=2)
+                for h in range(H):
+                    parts = []
+                    for bias_dram, mask_sb in ((attn_bias, adj_sb), (edge_bias, both_sb)):
+                        factor = work.tile([P, KT, IC], BF16, name="factor", bufs=3)
+                        nc.sync.dma_start(
+                            factor[:], bias_dram[b, h, :, lo : lo + IC].rearrange("(k p) i -> p k i", p=P)
+                        )
+                        nc.vector.tensor_tensor(factor[:], factor[:], mask_sb[:], ALU.mult)
+
+                        logits = work.tile([P, KT, IC], F32, name="logits", bufs=3)
+                        for kb in range(KT):
+                            s_ps = psum.tile([P, IC], F32, name="s_ps", bufs=2)
+                            nc.tensor.matmul(
+                                s_ps[:],
+                                lhsT=kh[:, h, b * T + kb * P : b * T + (kb + 1) * P],
+                                rhs=qh[:, h, b * T + lo : b * T + lo + IC],
+                                start=True,
+                                stop=True,
+                            )
+                            nc.vector.tensor_tensor(logits[:, kb, :], s_ps[:], factor[:, kb, :], ALU.mult)
+
+                        fold = work.tile([P, KT // 2, IC], F32, name="fold")
+                        nc.vector.tensor_tensor(fold[:], logits[:, 0 : KT // 2, :], logits[:, KT // 2 : KT, :], ALU.max)
+                        nc.vector.tensor_tensor(fold[:, 0:2, :], fold[:, 0:2, :], fold[:, 2:4, :], ALU.max)
+                        nc.vector.tensor_tensor(fold[:, 0, :], fold[:, 0, :], fold[:, 1, :], ALU.max)
+                        fold_t_ps = psum.tile([P, IB, P], F32, name="fold_t_ps")
+                        for ib in range(IB):
+                            nc.tensor.transpose(fold_t_ps[:, ib, :], fold[:, 0, ib * P : (ib + 1) * P], ident_f32[:])
+                        colmax = work.tile([P, IB], F32, name="colmax", bufs=2)
+                        nc.vector.reduce_max(colmax[:], fold_t_ps[:], axis=mybir.AxisListType.X)
+                        diag = work.tile([P, IB, P], F32, name="diag", bufs=2)
+                        for ib in range(IB):
+                            nc.scalar.activation(diag[:, ib, :], ident_f32[:], ACT.Copy, scale=colmax[:, ib : ib + 1])
+                        shift_ps = psum.tile([P, IC], F32, name="shift_ps")
+                        nc.tensor.matmul(
+                            shift_ps[:], lhsT=ones_f32[:], rhs=diag[:].rearrange("p a j -> p (a j)"), start=True, stop=True
+                        )
+                        shift = work.tile([P, IC], F32, name="shift", bufs=2)
+                        nc.scalar.activation(shift[:], shift_ps[:], ACT.Copy)
+
+                        nc.gpsimd.tensor_tensor(
+                            logits[:], logits[:], shift[:].unsqueeze(1).to_broadcast([P, KT, IC]), ALU.subtract
+                        )
+                        probs = work.tile([P, KT, IC], BF16, name="probs", bufs=2)
+                        nc.scalar.activation(probs[:], logits[:], ACT.Exp, scale=SCALE)
+
+                        part = work.tile([P, IB, DK], F32, name="part", bufs=4)
+                        parts.append(part)
+                        for ib in range(IB):
+                            o_ps = psum.tile([P, DK + 1], F32, name="o_ps", bufs=2)
+                            for kb in range(KT):
+                                nc.tensor.matmul(
+                                    o_ps[:],
+                                    lhsT=probs[:, kb, ib * P : (ib + 1) * P],
+                                    rhs=vaug[:, b * KT + kb, h, :],
+                                    start=(kb == 0),
+                                    stop=(kb == KT - 1),
+                                )
+                            recip = work.tile([P, 1], F32, name="recip", bufs=4)
+                            nc.vector.reciprocal(recip[:], o_ps[:, DK : DK + 1])
+                            nc.scalar.activation(part[:, ib, :], o_ps[:, 0:DK], ACT.Copy, scale=recip[:])
+                    nc.gpsimd.tensor_tensor(att_t[:, :, h * DK : (h + 1) * DK], parts[0][:], parts[1][:], ALU.add)
+
+                att = work.tile([P, CB, IC], BF16, name="att", bufs=2)
+                for e in range(CB):
+                    att_ps = psum.tile([P, IB, P], BF16, name="att_ps")
+                    for ib in range(IB):
+                        nc.tensor.transpose(att_ps[:, ib, :], att_t[:, ib, e * P : (e + 1) * P], ident_bf16[:])
+                    nc.scalar.activation(att[:, e, :], att_ps[:].rearrange("p a j -> p (a j)"), ACT.Copy)
+                for cb in range(CB):
+                    y_ps = psum.tile([P, IC], F32, name="y_ps")
+                    for e in range(CB):
+                        nc.tensor.matmul(
+                            y_ps[:],
+                            lhsT=weights["wo"][:, e, cb * P : (cb + 1) * P],
+                            rhs=att[:, e, :],
+                            start=(e == 0),
+                            stop=(e == CB - 1),
+                        )
+                    nc.scalar.activation(y_sb[cb][:, b * T + lo : b * T + lo + IC], y_ps[:], ACT.Copy)
+
+        for cb in range(CB):
+            window = windows[cb]
+            nc.sync.dma_start(window[:], base[cb * P : (cb + 1) * P, :])
+            nc.vector.tensor_tensor(
+                window[:].indirect(offsets[:]),
+                y_sb[cb][:],
+                bo_wide[cb][:],
+                ALU.add,
+            )
+            nc.sync.dma_start(out[cb * P : (cb + 1) * P, :], window[:])

@@ -6,15 +6,18 @@ from concourse.masks import make_identity
 BF16, F32, U16 = mybir.dt.bfloat16, mybir.dt.float32, mybir.dt.uint16
 ALU = mybir.AluOpType
 ACT = mybir.ActivationFunctionType
+AXIS_X = mybir.AxisListType.X
 
 P = 128
 B, T, C, H, DK, S, N = 2, 1024, 256, 2, 128, 4096, 2048
 SCALE = 32.0**-0.5
 CB = C // P
 KT = T // P
-IC = 512
-NCH = T // IC
+BANK = 512
+IC = BANK
 IB = IC // P
+HALVES = T // BANK
+KH = KT // HALVES
 
 FLOPS = 4 * 2 * C * C * N + 3 * B * H * 2 * DK * T * T
 
@@ -25,7 +28,8 @@ def tile_multiheadattention_b_kernel(
     nc = tc.nc
     with ExitStack() as ctx:
         held = ctx.enter_context(tc.tile_pool(name="held", bufs=1))
-        work = ctx.enter_context(tc.tile_pool(name="work", bufs=1))
+        work = ctx.enter_context(tc.tile_pool(name="work", bufs=2))
+        psum = ctx.enter_context(tc.psum_pool(name="psum", bufs=2))
 
         offsets = held.tile([P, N // 16], U16, name="offsets")
         nc.sync.dma_start(offsets[:], offs)
@@ -34,112 +38,95 @@ def tile_multiheadattention_b_kernel(
         make_identity(nc, ident_f32[:])
         ident_bf16 = held.tile([P, P], BF16, name="ident_bf16")
         make_identity(nc, ident_bf16[:])
-        ones_f32 = held.tile([P, P], F32, name="ones_f32")
-        nc.vector.memset(ones_f32[:], 1.0)
 
         weights = {}
         for name, w_dram in (("wk", wk), ("wq", wq), ("wv", wv), ("wo", wo)):
             weights[name] = held.tile([P, CB, C], BF16, name=name)
             nc.sync.dma_start(weights[name][:], w_dram.rearrange("(e p) c -> p e c", p=P))
 
+        bias_rows = held.tile([3 * CB, P], F32, name="bias_rows")
+        for j, b_dram in enumerate((bq, bk, bo)):
+            nc.sync.dma_start(bias_rows[j * CB : (j + 1) * CB, :], b_dram.rearrange("(e p) one -> e (p one)", p=P))
+        bias_ps = psum.tile([P, 3 * CB], F32, name="bias_ps", tag="sums")
+        nc.tensor.matmul(bias_ps[:], lhsT=bias_rows[:], rhs=ident_f32[0 : 3 * CB, 0 : 3 * CB], start=True, stop=True)
+        bias_cols = held.tile([P, 3 * CB], F32, name="bias_cols")
+        nc.vector.tensor_copy(bias_cols[:], bias_ps[:])
+        bv_all = held.tile([P, C], F32, name="bv_all")
+        nc.sync.dma_start(bv_all[:], bv.rearrange("c one -> (c one)").partition_broadcast(P))
+
         windows = [held.tile([P, S], F32, name=f"window{cb}") for cb in range(CB)]
+        y_sb = [held.tile([P, N], F32, name=f"y_sb{cb}") for cb in range(CB)]
 
         qh = held.tile([P, H, N], BF16, name="qh")
         kh = held.tile([P, H, N], BF16, name="kh")
         vaug = held.tile([P, B * KT, H, DK + 1], BF16, name="vaug")
-        bias_cols = held.tile([P, 3 * CB], F32, name="bias_cols")
-        bv_all = held.tile([P, C], F32, name="bv_all")
-        nc.sync.dma_start(bv_all[:], bv.rearrange("c one -> (c one)").partition_broadcast(P))
+        nc.vector.memset(vaug[:, :, :, DK : DK + 1], 1.0)
 
-        with (
-            tc.tile_pool(name="stage", bufs=1) as stage,
-            tc.psum_pool(name="proj_psum", bufs=2) as proj_psum,
-        ):
-            bias_rows = stage.tile([1, 3 * C], F32, name="bias_rows")
-            for j, b_dram in enumerate((bq, bk, bo)):
-                nc.sync.dma_start(bias_rows[0:1, j * C : (j + 1) * C], b_dram.rearrange("c one -> one c"))
-            one = stage.tile([1, 1], F32, name="one")
-            nc.vector.memset(one[:], 1.0)
-            bias_ps = proj_psum.tile([P, 3 * CB], F32, name="bias_ps")
-            for j in range(3 * CB):
-                nc.tensor.matmul(
-                    bias_ps[:, j : j + 1], lhsT=bias_rows[0:1, j * P : (j + 1) * P], rhs=one[:], start=True, stop=True
-                )
-            nc.vector.tensor_copy(bias_cols[:], bias_ps[:])
-
+        for b in range(B):
             staged = {}
             for name, x_dram in (("k", k), ("q", q), ("v", v)):
-                staged[name] = stage.tile([P, CB, N], BF16, name=name + "_sb")
-                nc.sync.dma_start(staged[name][:], x_dram.rearrange("(e p) n -> p e n", p=P))
+                staged[name] = work.tile([P, CB, T], BF16, name=name + "_sb", bufs=1)
+                nc.sync.dma_start(
+                    staged[name][:], x_dram[:, b * T : (b + 1) * T].rearrange("(e p) n -> p e n", p=P)
+                )
 
             for dst, w_sb, x_sb, first_col in ((kh, weights["wk"], staged["k"], CB), (qh, weights["wq"], staged["q"], 0)):
                 for h in range(H):
-                    for n in range(N // IC):
-                        proj_ps = proj_psum.tile([P, IC], F32, name="proj_ps")
+                    for n in range(T // BANK):
+                        proj_ps = psum.tile([P, BANK], F32, name="proj_ps", tag="rows")
                         for e in range(CB):
                             nc.tensor.matmul(
                                 proj_ps[:],
                                 lhsT=w_sb[:, e, h * P : (h + 1) * P],
-                                rhs=x_sb[:, e, n * IC : (n + 1) * IC],
+                                rhs=x_sb[:, e, n * BANK : (n + 1) * BANK],
                                 start=(e == 0),
                                 stop=(e == CB - 1),
                             )
                         nc.scalar.activation(
-                            dst[:, h, n * IC : (n + 1) * IC],
+                            dst[:, h, b * T + n * BANK : b * T + (n + 1) * BANK],
                             proj_ps[:],
                             ACT.Identity,
                             bias=bias_cols[:, first_col + h : first_col + h + 1],
                         )
 
-            nc.vector.memset(vaug[:, :, :, DK : DK + 1], 1.0)
-            for tb in range(B * KT):
-                v_ps = proj_psum.tile([P, C], F32, name="v_ps")
+            for kb in range(KT):
+                v_ps = psum.tile([P, C], F32, name="v_ps", tag="rows")
                 for e in range(CB):
                     nc.tensor.matmul(
                         v_ps[:],
-                        lhsT=staged["v"][:, e, tb * P : (tb + 1) * P],
+                        lhsT=staged["v"][:, e, kb * P : (kb + 1) * P],
                         rhs=weights["wv"][:, e, :],
                         start=(e == 0),
                         stop=(e == CB - 1),
                     )
                 nc.vector.tensor_tensor(
-                    vaug[:, tb, :, 0:DK],
+                    vaug[:, b * KT + kb, :, 0:DK],
                     v_ps[:].rearrange("p (h d) -> p h d", h=H),
                     bv_all[:].rearrange("p (h d) -> p h d", h=H),
                     ALU.add,
                 )
 
-        late = ctx.enter_context(tc.tile_pool(name="late", bufs=1))
-        psum = ctx.enter_context(tc.psum_pool(name="psum", bufs=1))
-        y_sb = [late.tile([P, N], F32, name=f"y_sb{cb}") for cb in range(CB)]
-        bo_wide = [late.tile([P, N], F32, name=f"bo_wide{cb}") for cb in range(CB)]
-        for cb in range(CB):
-            nc.scalar.activation(
-                bo_wide[cb][:], bias_cols[:, 2 * CB + cb : 2 * CB + cb + 1].to_broadcast([P, N]), ACT.Copy
-            )
-
-        for b in range(B):
-            for ch in range(NCH):
-                lo = ch * IC
+            for lo in range(0, T, IC):
                 adj_sb = work.tile([P, KT, IC], BF16, name="adj_sb")
                 nc.sync.dma_start(adj_sb[:], adj[b, :, lo : lo + IC].rearrange("(k p) i -> p k i", p=P))
                 both_sb = work.tile([P, KT, IC], BF16, name="both_sb")
                 nc.sync.dma_start(both_sb[:], adj1[b, :, lo : lo + IC].rearrange("(k p) i -> p k i", p=P))
-                nc.vector.tensor_tensor(both_sb[:], both_sb[:], adj_sb[:], ALU.mult)
 
-                att_t = work.tile([P, IB, C], BF16, name="att_t", bufs=2)
-                for h in range(H):
-                    parts = []
-                    for bias_dram, mask_sb in ((attn_bias, adj_sb), (edge_bias, both_sb)):
+                att_t = work.tile([P, IB, C], BF16, name="att_t")
+                first_part = work.tile([P, IB, C], F32, name="first_part")
+                for branch, (bias_dram, mask_sb) in enumerate(((attn_bias, adj_sb), (edge_bias, both_sb))):
+                    if branch == 1:
+                        nc.gpsimd.tensor_tensor(both_sb[:], both_sb[:], adj_sb[:], ALU.mult)
+                    for h in range(H):
                         factor = work.tile([P, KT, IC], BF16, name="factor", bufs=3)
                         nc.sync.dma_start(
                             factor[:], bias_dram[b, h, :, lo : lo + IC].rearrange("(k p) i -> p k i", p=P)
                         )
-                        nc.vector.tensor_tensor(factor[:], factor[:], mask_sb[:], ALU.mult)
+                        nc.gpsimd.tensor_tensor(factor[:], factor[:], mask_sb[:], ALU.mult)
 
                         logits = work.tile([P, KT, IC], F32, name="logits", bufs=3)
                         for kb in range(KT):
-                            s_ps = psum.tile([P, IC], F32, name="s_ps", bufs=2)
+                            s_ps = psum.tile([P, IC], F32, name="s_ps", tag="raw")
                             nc.tensor.matmul(
                                 s_ps[:],
                                 lhsT=kh[:, h, b * T + kb * P : b * T + (kb + 1) * P],
@@ -149,56 +136,69 @@ def tile_multiheadattention_b_kernel(
                             )
                             nc.vector.tensor_tensor(logits[:, kb, :], s_ps[:], factor[:, kb, :], ALU.mult)
 
-                        fold = work.tile([P, KT // 2, IC], F32, name="fold")
-                        nc.vector.tensor_tensor(fold[:], logits[:, 0 : KT // 2, :], logits[:, KT // 2 : KT, :], ALU.max)
-                        nc.vector.tensor_tensor(fold[:, 0:2, :], fold[:, 0:2, :], fold[:, 2:4, :], ALU.max)
-                        nc.vector.tensor_tensor(fold[:, 0, :], fold[:, 0, :], fold[:, 1, :], ALU.max)
-                        fold_t_ps = psum.tile([P, IB, P], F32, name="fold_t_ps")
                         for ib in range(IB):
-                            nc.tensor.transpose(fold_t_ps[:, ib, :], fold[:, 0, ib * P : (ib + 1) * P], ident_f32[:])
-                        colmax = work.tile([P, IB], F32, name="colmax", bufs=2)
-                        nc.vector.reduce_max(colmax[:], fold_t_ps[:], axis=mybir.AxisListType.X)
-                        diag = work.tile([P, IB, P], F32, name="diag", bufs=2)
-                        for ib in range(IB):
-                            nc.scalar.activation(diag[:, ib, :], ident_f32[:], ACT.Copy, scale=colmax[:, ib : ib + 1])
-                        shift_ps = psum.tile([P, IC], F32, name="shift_ps")
-                        nc.tensor.matmul(
-                            shift_ps[:], lhsT=ones_f32[:], rhs=diag[:].rearrange("p a j -> p (a j)"), start=True, stop=True
-                        )
-                        shift = work.tile([P, IC], F32, name="shift", bufs=2)
-                        nc.scalar.activation(shift[:], shift_ps[:], ACT.Copy)
+                            rows_sb = work.tile([P, T], F32, name="rows_sb", bufs=3)
+                            half_max = work.tile([P, HALVES], F32, name="half_max", bufs=4)
+                            for half in range(HALVES):
+                                rows_ps = psum.tile([P, BANK], F32, name="rows_ps", tag="rows")
+                                for kk in range(KH):
+                                    nc.tensor.transpose(
+                                        rows_ps[:, kk * P : (kk + 1) * P],
+                                        logits[:, half * KH + kk, ib * P : (ib + 1) * P],
+                                        ident_f32[:],
+                                    )
+                                nc.vector.tensor_scalar(
+                                    rows_sb[:, half * BANK : (half + 1) * BANK],
+                                    rows_ps[:],
+                                    SCALE,
+                                    None,
+                                    op0=ALU.mult,
+                                    op1=ALU.max,
+                                    accum_out=half_max[:, half : half + 1],
+                                )
+                            shift = work.tile([P, 1], F32, name="shift", bufs=4)
+                            nc.vector.reduce_max(shift[:], half_max[:], axis=AXIS_X, negate=True)
+                            probs_t = work.tile([P, T], BF16, name="probs_t", bufs=3)
+                            nc.scalar.activation(probs_t[:], rows_sb[:], ACT.Exp, bias=shift[:])
+                            probs_ps = psum.tile([P, KT, P], BF16, name="probs_ps", tag="back")
+                            for kb in range(KT):
+                                nc.tensor.transpose(probs_ps[:, kb, :], probs_t[:, kb * P : (kb + 1) * P], ident_bf16[:])
+                            probs = work.tile([P, KT, P], BF16, name="probs", bufs=3)
+                            nc.scalar.activation(probs[:], probs_ps[:], ACT.Copy)
 
-                        nc.gpsimd.tensor_tensor(
-                            logits[:], logits[:], shift[:].unsqueeze(1).to_broadcast([P, KT, IC]), ALU.subtract
-                        )
-                        probs = work.tile([P, KT, IC], BF16, name="probs", bufs=2)
-                        nc.scalar.activation(probs[:], logits[:], ACT.Exp, scale=SCALE)
-
-                        part = work.tile([P, IB, DK], F32, name="part", bufs=4)
-                        parts.append(part)
-                        for ib in range(IB):
-                            o_ps = psum.tile([P, DK + 1], F32, name="o_ps", bufs=2)
+                            o_ps = psum.tile([P, DK + 1], F32, name="o_ps", tag="sums")
                             for kb in range(KT):
                                 nc.tensor.matmul(
                                     o_ps[:],
-                                    lhsT=probs[:, kb, ib * P : (ib + 1) * P],
+                                    lhsT=probs[:, kb, :],
                                     rhs=vaug[:, b * KT + kb, h, :],
                                     start=(kb == 0),
                                     stop=(kb == KT - 1),
                                 )
                             recip = work.tile([P, 1], F32, name="recip", bufs=4)
                             nc.vector.reciprocal(recip[:], o_ps[:, DK : DK + 1])
-                            nc.scalar.activation(part[:, ib, :], o_ps[:, 0:DK], ACT.Copy, scale=recip[:])
-                    nc.gpsimd.tensor_tensor(att_t[:, :, h * DK : (h + 1) * DK], parts[0][:], parts[1][:], ALU.add)
+                            if branch == 0:
+                                nc.scalar.activation(
+                                    first_part[:, ib, h * DK : (h + 1) * DK], o_ps[:, 0:DK], ACT.Copy, scale=recip[:]
+                                )
+                            else:
+                                nc.vector.scalar_tensor_tensor(
+                                    att_t[:, ib, h * DK : (h + 1) * DK],
+                                    in0=o_ps[:, 0:DK],
+                                    scalar=recip[:],
+                                    in1=first_part[:, ib, h * DK : (h + 1) * DK],
+                                    op0=ALU.mult,
+                                    op1=ALU.add,
+                                )
 
-                att = work.tile([P, CB, IC], BF16, name="att", bufs=2)
+                att = work.tile([P, CB, IC], BF16, name="att")
                 for e in range(CB):
-                    att_ps = psum.tile([P, IB, P], BF16, name="att_ps")
+                    att_ps = psum.tile([P, IB, P], BF16, name="att_ps", tag="back")
                     for ib in range(IB):
                         nc.tensor.transpose(att_ps[:, ib, :], att_t[:, ib, e * P : (e + 1) * P], ident_bf16[:])
                     nc.scalar.activation(att[:, e, :], att_ps[:].rearrange("p a j -> p (a j)"), ACT.Copy)
                 for cb in range(CB):
-                    y_ps = psum.tile([P, IC], F32, name="y_ps")
+                    y_ps = psum.tile([P, IC], F32, name="y_ps", tag="raw")
                     for e in range(CB):
                         nc.tensor.matmul(
                             y_ps[:],
@@ -212,10 +212,7 @@ def tile_multiheadattention_b_kernel(
         for cb in range(CB):
             window = windows[cb]
             nc.sync.dma_start(window[:], base[cb * P : (cb + 1) * P, :])
-            nc.vector.tensor_tensor(
-                window[:].indirect(offsets[:]),
-                y_sb[cb][:],
-                bo_wide[cb][:],
-                ALU.add,
-            )
+            bo_wide = work.tile([P, N], F32, name="bo_wide", tag="logits", bufs=3)
+            nc.scalar.activation(bo_wide[:], bias_cols[:, 2 * CB + cb : 2 * CB + cb + 1].to_broadcast([P, N]), ACT.Copy)
+            nc.vector.tensor_tensor(window[:].indirect(offsets[:]), y_sb[cb][:], bo_wide[:], ALU.add)
             nc.sync.dma_start(out[cb * P : (cb + 1) * P, :], window[:])

@@ -11,6 +11,7 @@ AXIS_X = mybir.AxisListType.X
 P = 128
 B, T, C, H, DK, S, N = 2, 1024, 256, 2, 128, 4096, 2048
 SCALE = 32.0**-0.5
+BRANCHES = 2
 CB = C // P
 KT = T // P
 BANK = 512
@@ -18,6 +19,7 @@ IC = BANK
 IB = IC // P
 HALVES = T // BANK
 KH = KT // HALVES
+PIECE = 2
 
 FLOPS = 4 * 2 * C * C * N + 3 * B * H * 2 * DK * T * T
 
@@ -47,20 +49,17 @@ def tile_multiheadattention_b_kernel(
         bias_rows = held.tile([3 * CB, P], F32, name="bias_rows")
         for j, b_dram in enumerate((bq, bk, bo)):
             nc.sync.dma_start(bias_rows[j * CB : (j + 1) * CB, :], b_dram.rearrange("(e p) one -> e (p one)", p=P))
-        bias_ps = psum.tile([P, 3 * CB], F32, name="bias_ps", tag="sums")
+        bias_ps = psum.tile([P, 3 * CB], F32, name="bias_ps", tag="acc", bufs=1)
         nc.tensor.matmul(bias_ps[:], lhsT=bias_rows[:], rhs=ident_f32[0 : 3 * CB, 0 : 3 * CB], start=True, stop=True)
         bias_cols = held.tile([P, 3 * CB], F32, name="bias_cols")
         nc.vector.tensor_copy(bias_cols[:], bias_ps[:])
         bv_all = held.tile([P, C], F32, name="bv_all")
         nc.sync.dma_start(bv_all[:], bv.rearrange("c one -> (c one)").partition_broadcast(P))
 
-        windows = [held.tile([P, S], F32, name=f"window{cb}") for cb in range(CB)]
         y_sb = [held.tile([P, N], F32, name=f"y_sb{cb}") for cb in range(CB)]
-
         qh = held.tile([P, H, N], BF16, name="qh")
         kh = held.tile([P, H, N], BF16, name="kh")
-        vaug = held.tile([P, B * KT, H, DK + 1], BF16, name="vaug")
-        nc.vector.memset(vaug[:, :, :, DK : DK + 1], 1.0)
+        vh_t = held.tile([P, B * KT, C], BF16, name="vh_t")
 
         for b in range(B):
             staged = {}
@@ -70,10 +69,10 @@ def tile_multiheadattention_b_kernel(
                     staged[name][:], x_dram[:, b * T : (b + 1) * T].rearrange("(e p) n -> p e n", p=P)
                 )
 
-            for dst, w_sb, x_sb, first_col in ((kh, weights["wk"], staged["k"], CB), (qh, weights["wq"], staged["q"], 0)):
-                for h in range(H):
+            for h in range(H):
+                for dst, w_sb, x_sb, first_col in ((kh, weights["wk"], staged["k"], CB), (qh, weights["wq"], staged["q"], 0)):
                     for n in range(T // BANK):
-                        proj_ps = psum.tile([P, BANK], F32, name="proj_ps", tag="rows")
+                        proj_ps = psum.tile([P, BANK], F32, name="proj_ps", tag="rows", bufs=3)
                         for e in range(CB):
                             nc.tensor.matmul(
                                 proj_ps[:],
@@ -90,7 +89,7 @@ def tile_multiheadattention_b_kernel(
                         )
 
             for kb in range(KT):
-                v_ps = psum.tile([P, C], F32, name="v_ps", tag="rows")
+                v_ps = psum.tile([P, C], F32, name="v_ps", tag="rows", bufs=3)
                 for e in range(CB):
                     nc.tensor.matmul(
                         v_ps[:],
@@ -99,52 +98,64 @@ def tile_multiheadattention_b_kernel(
                         start=(e == 0),
                         stop=(e == CB - 1),
                     )
-                nc.vector.tensor_tensor(
-                    vaug[:, b * KT + kb, :, 0:DK],
-                    v_ps[:].rearrange("p (h d) -> p h d", h=H),
-                    bv_all[:].rearrange("p (h d) -> p h d", h=H),
-                    ALU.add,
-                )
+                nc.vector.tensor_tensor(vh_t[:, b * KT + kb, :], v_ps[:], bv_all[:], ALU.add)
 
             for lo in range(0, T, IC):
                 adj_sb = work.tile([P, KT, IC], BF16, name="adj_sb")
-                nc.sync.dma_start(adj_sb[:], adj[b, :, lo : lo + IC].rearrange("(k p) i -> p k i", p=P))
                 both_sb = work.tile([P, KT, IC], BF16, name="both_sb")
-                nc.sync.dma_start(both_sb[:], adj1[b, :, lo : lo + IC].rearrange("(k p) i -> p k i", p=P))
 
-                att_t = work.tile([P, IB, C], BF16, name="att_t")
-                first_part = work.tile([P, IB, C], F32, name="first_part")
-                for branch, (bias_dram, mask_sb) in enumerate(((attn_bias, adj_sb), (edge_bias, both_sb))):
-                    if branch == 1:
-                        nc.gpsimd.tensor_tensor(both_sb[:], both_sb[:], adj_sb[:], ALU.mult)
-                    for h in range(H):
-                        factor = work.tile([P, KT, IC], BF16, name="factor", bufs=3)
-                        nc.sync.dma_start(
-                            factor[:], bias_dram[b, h, :, lo : lo + IC].rearrange("(k p) i -> p k i", p=P)
-                        )
-                        nc.gpsimd.tensor_tensor(factor[:], factor[:], mask_sb[:], ALU.mult)
-
-                        logits = work.tile([P, KT, IC], F32, name="logits", bufs=3)
-                        for kb in range(KT):
-                            s_ps = psum.tile([P, IC], F32, name="s_ps", tag="raw")
-                            nc.tensor.matmul(
-                                s_ps[:],
-                                lhsT=kh[:, h, b * T + kb * P : b * T + (kb + 1) * P],
-                                rhs=qh[:, h, b * T + lo : b * T + lo + IC],
-                                start=True,
-                                stop=True,
+                att = work.tile([P, H, IC], BF16, name="att")
+                for h in range(H):
+                    factors = [work.tile([P, KT, IC], BF16, name="factor", bufs=4) for branch in range(BRANCHES)]
+                    loads = [(factors[0], attn_bias[b, h]), (factors[1], edge_bias[b, h])]
+                    if h == 0:
+                        loads = [(adj_sb, adj[b]), (both_sb, adj1[b])] + loads
+                    for k0 in range(0, KT, PIECE):
+                        for tile_sb, x_dram in loads:
+                            nc.sync.dma_start(
+                                tile_sb[:, k0 : k0 + PIECE, :],
+                                x_dram[k0 * P : (k0 + PIECE) * P, lo : lo + IC].rearrange("(k p) i -> p k i", p=P),
                             )
-                            nc.vector.tensor_tensor(logits[:, kb, :], s_ps[:], factor[:, kb, :], ALU.mult)
+                        if h == 0:
+                            nc.vector.tensor_tensor(
+                                both_sb[:, k0 : k0 + PIECE, :],
+                                both_sb[:, k0 : k0 + PIECE, :],
+                                adj_sb[:, k0 : k0 + PIECE, :],
+                                ALU.mult,
+                            )
+                        for factor, mask_sb in zip(factors, (adj_sb, both_sb)):
+                            nc.gpsimd.tensor_tensor(
+                                factor[:, k0 : k0 + PIECE, :],
+                                factor[:, k0 : k0 + PIECE, :],
+                                mask_sb[:, k0 : k0 + PIECE, :],
+                                ALU.mult,
+                            )
 
+                    logits = [work.tile([P, KT, IC], F32, name="logits", bufs=4) for branch in range(BRANCHES)]
+                    for kb in range(KT):
+                        s_ps = psum.tile([P, IC], F32, name="s_ps", tag="raw")
+                        nc.tensor.matmul(
+                            s_ps[:],
+                            lhsT=kh[:, h, b * T + kb * P : b * T + (kb + 1) * P],
+                            rhs=qh[:, h, b * T + lo : b * T + lo + IC],
+                            start=True,
+                            stop=True,
+                        )
+                        for branch in range(BRANCHES):
+                            nc.vector.tensor_tensor(logits[branch][:, kb, :], s_ps[:], factors[branch][:, kb, :], ALU.mult)
+
+                    acc_ps = psum.tile([P, IC], F32, name="acc_ps", tag="acc", bufs=1)
+                    for branch in range(BRANCHES):
+                        probs = work.tile([P, KT, IC], BF16, name="probs")
                         for ib in range(IB):
                             rows_sb = work.tile([P, T], F32, name="rows_sb", bufs=3)
                             half_max = work.tile([P, HALVES], F32, name="half_max", bufs=4)
                             for half in range(HALVES):
-                                rows_ps = psum.tile([P, BANK], F32, name="rows_ps", tag="rows")
+                                rows_ps = psum.tile([P, BANK], F32, name="rows_ps", tag="rows", bufs=3)
                                 for kk in range(KH):
                                     nc.tensor.transpose(
                                         rows_ps[:, kk * P : (kk + 1) * P],
-                                        logits[:, half * KH + kk, ib * P : (ib + 1) * P],
+                                        logits[branch][:, half * KH + kk, ib * P : (ib + 1) * P],
                                         ident_f32[:],
                                     )
                                 nc.vector.tensor_scalar(
@@ -158,61 +169,45 @@ def tile_multiheadattention_b_kernel(
                                 )
                             shift = work.tile([P, 1], F32, name="shift", bufs=4)
                             nc.vector.reduce_max(shift[:], half_max[:], axis=AXIS_X, negate=True)
-                            probs_t = work.tile([P, T], BF16, name="probs_t", bufs=3)
-                            nc.scalar.activation(probs_t[:], rows_sb[:], ACT.Exp, bias=shift[:])
-                            probs_ps = psum.tile([P, KT, P], BF16, name="probs_ps", tag="back")
-                            for kb in range(KT):
-                                nc.tensor.transpose(probs_ps[:, kb, :], probs_t[:, kb * P : (kb + 1) * P], ident_bf16[:])
-                            probs = work.tile([P, KT, P], BF16, name="probs", bufs=3)
-                            nc.scalar.activation(probs[:], probs_ps[:], ACT.Copy)
-
-                            o_ps = psum.tile([P, DK + 1], F32, name="o_ps", tag="sums")
+                            expo_t = work.tile([P, T], BF16, name="expo_t", bufs=3)
+                            row_sum = work.tile([P, 1], F32, name="row_sum", bufs=4)
+                            nc.scalar.activation(expo_t[:], rows_sb[:], ACT.Exp, bias=shift[:], accum_out=row_sum[:])
+                            recip = work.tile([P, 1], F32, name="recip", bufs=4)
+                            nc.vector.reciprocal(recip[:], row_sum[:])
+                            diag = work.tile([P, P], BF16, name="diag", bufs=3)
+                            nc.scalar.activation(diag[:], ident_bf16[:], ACT.Copy, scale=recip[:])
+                            back_ps = psum.tile([P, KT, P], BF16, name="back_ps", tag="back")
                             for kb in range(KT):
                                 nc.tensor.matmul(
-                                    o_ps[:],
-                                    lhsT=probs[:, kb, :],
-                                    rhs=vaug[:, b * KT + kb, h, :],
-                                    start=(kb == 0),
-                                    stop=(kb == KT - 1),
+                                    back_ps[:, kb, :], lhsT=expo_t[:, kb * P : (kb + 1) * P], rhs=diag[:], start=True, stop=True
                                 )
-                            recip = work.tile([P, 1], F32, name="recip", bufs=4)
-                            nc.vector.reciprocal(recip[:], o_ps[:, DK : DK + 1])
-                            if branch == 0:
-                                nc.scalar.activation(
-                                    first_part[:, ib, h * DK : (h + 1) * DK], o_ps[:, 0:DK], ACT.Copy, scale=recip[:]
-                                )
-                            else:
-                                nc.vector.scalar_tensor_tensor(
-                                    att_t[:, ib, h * DK : (h + 1) * DK],
-                                    in0=o_ps[:, 0:DK],
-                                    scalar=recip[:],
-                                    in1=first_part[:, ib, h * DK : (h + 1) * DK],
-                                    op0=ALU.mult,
-                                    op1=ALU.add,
-                                )
+                            nc.scalar.activation(probs[:, :, ib * P : (ib + 1) * P], back_ps[:], ACT.Copy)
+                        for kb in range(KT):
+                            nc.tensor.matmul(
+                                acc_ps[:],
+                                lhsT=vh_t[:, b * KT + kb, h * DK : (h + 1) * DK],
+                                rhs=probs[:, kb, :],
+                                start=(branch == 0 and kb == 0),
+                                stop=(branch == BRANCHES - 1 and kb == KT - 1),
+                            )
+                    nc.scalar.activation(att[:, h, :], acc_ps[:], ACT.Copy)
 
-                att = work.tile([P, CB, IC], BF16, name="att")
-                for e in range(CB):
-                    att_ps = psum.tile([P, IB, P], BF16, name="att_ps", tag="back")
-                    for ib in range(IB):
-                        nc.tensor.transpose(att_ps[:, ib, :], att_t[:, ib, e * P : (e + 1) * P], ident_bf16[:])
-                    nc.scalar.activation(att[:, e, :], att_ps[:].rearrange("p a j -> p (a j)"), ACT.Copy)
                 for cb in range(CB):
-                    y_ps = psum.tile([P, IC], F32, name="y_ps", tag="raw")
-                    for e in range(CB):
+                    y_ps = psum.tile([P, IC], F32, name="y_ps", tag="acc", bufs=1)
+                    for h in range(H):
                         nc.tensor.matmul(
                             y_ps[:],
-                            lhsT=weights["wo"][:, e, cb * P : (cb + 1) * P],
-                            rhs=att[:, e, :],
-                            start=(e == 0),
-                            stop=(e == CB - 1),
+                            lhsT=weights["wo"][:, h, cb * P : (cb + 1) * P],
+                            rhs=att[:, h, :],
+                            start=(h == 0),
+                            stop=(h == H - 1),
                         )
                     nc.scalar.activation(y_sb[cb][:, b * T + lo : b * T + lo + IC], y_ps[:], ACT.Copy)
 
         for cb in range(CB):
-            window = windows[cb]
+            window = work.tile([P, S], F32, name="window", tag="logits", bufs=4)
             nc.sync.dma_start(window[:], base[cb * P : (cb + 1) * P, :])
-            bo_wide = work.tile([P, N], F32, name="bo_wide", tag="logits", bufs=3)
+            bo_wide = work.tile([P, N], F32, name="bo_wide", tag="factor", bufs=4)
             nc.scalar.activation(bo_wide[:], bias_cols[:, 2 * CB + cb : 2 * CB + cb + 1].to_broadcast([P, N]), ACT.Copy)
             nc.vector.tensor_tensor(window[:].indirect(offsets[:]), y_sb[cb][:], bo_wide[:], ALU.add)
             nc.sync.dma_start(out[cb * P : (cb + 1) * P, :], window[:])

@@ -102,27 +102,21 @@ def tile_multiheadattention_b_kernel(
 
             for lo in range(0, T, IC):
                 adj_sb = work.tile([P, KT, IC], BF16, name="adj_sb")
+                nc.sync.dma_start(adj_sb[:], adj[b, :, lo : lo + IC].rearrange("(k p) i -> p k i", p=P))
                 both_sb = work.tile([P, KT, IC], BF16, name="both_sb")
+                nc.sync.dma_start(both_sb[:], adj1[b, :, lo : lo + IC].rearrange("(k p) i -> p k i", p=P))
+                nc.vector.tensor_tensor(both_sb[:], both_sb[:], adj_sb[:], ALU.mult)
 
                 att = work.tile([P, H, IC], BF16, name="att")
                 for h in range(H):
-                    factors = [work.tile([P, KT, IC], BF16, name="factor", bufs=4) for branch in range(BRANCHES)]
-                    loads = [(factors[0], attn_bias[b, h]), (factors[1], edge_bias[b, h])]
-                    if h == 0:
-                        loads = [(adj_sb, adj[b]), (both_sb, adj1[b])] + loads
+                    factors = []
+                    for bias_dram in (attn_bias, edge_bias):
+                        factor = work.tile([P, KT, IC], BF16, name="factor", bufs=4)
+                        nc.sync.dma_start(
+                            factor[:], bias_dram[b, h, :, lo : lo + IC].rearrange("(k p) i -> p k i", p=P)
+                        )
+                        factors.append(factor)
                     for k0 in range(0, KT, PIECE):
-                        for tile_sb, x_dram in loads:
-                            nc.sync.dma_start(
-                                tile_sb[:, k0 : k0 + PIECE, :],
-                                x_dram[k0 * P : (k0 + PIECE) * P, lo : lo + IC].rearrange("(k p) i -> p k i", p=P),
-                            )
-                        if h == 0:
-                            nc.vector.tensor_tensor(
-                                both_sb[:, k0 : k0 + PIECE, :],
-                                both_sb[:, k0 : k0 + PIECE, :],
-                                adj_sb[:, k0 : k0 + PIECE, :],
-                                ALU.mult,
-                            )
                         for factor, mask_sb in zip(factors, (adj_sb, both_sb)):
                             nc.gpsimd.tensor_tensor(
                                 factor[:, k0 : k0 + PIECE, :],
@@ -146,9 +140,9 @@ def tile_multiheadattention_b_kernel(
 
                     acc_ps = psum.tile([P, IC], F32, name="acc_ps", tag="acc", bufs=1)
                     for branch in range(BRANCHES):
-                        probs = work.tile([P, KT, IC], BF16, name="probs")
+                        probs = work.tile([P, KT, IC], BF16, name="probs", bufs=3)
                         for ib in range(IB):
-                            rows_sb = work.tile([P, T], F32, name="rows_sb", bufs=3)
+                            rows_sb = work.tile([P, T], F32, name="rows_sb", bufs=4)
                             half_max = work.tile([P, HALVES], F32, name="half_max", bufs=4)
                             for half in range(HALVES):
                                 rows_ps = psum.tile([P, BANK], F32, name="rows_ps", tag="rows", bufs=3)
@@ -174,14 +168,14 @@ def tile_multiheadattention_b_kernel(
                             nc.scalar.activation(expo_t[:], rows_sb[:], ACT.Exp, bias=shift[:], accum_out=row_sum[:])
                             recip = work.tile([P, 1], F32, name="recip", bufs=4)
                             nc.vector.reciprocal(recip[:], row_sum[:])
-                            diag = work.tile([P, P], BF16, name="diag", bufs=3)
+                            diag = work.tile([P, P], BF16, name="diag", bufs=4)
                             nc.scalar.activation(diag[:], ident_bf16[:], ACT.Copy, scale=recip[:])
                             back_ps = psum.tile([P, KT, P], BF16, name="back_ps", tag="back")
                             for kb in range(KT):
                                 nc.tensor.matmul(
                                     back_ps[:, kb, :], lhsT=expo_t[:, kb * P : (kb + 1) * P], rhs=diag[:], start=True, stop=True
                                 )
-                            nc.scalar.activation(probs[:, :, ib * P : (ib + 1) * P], back_ps[:], ACT.Copy)
+                            nc.scalar.copy(probs[:, :, ib * P : (ib + 1) * P], back_ps[:])
                         for kb in range(KT):
                             nc.tensor.matmul(
                                 acc_ps[:],

@@ -6,20 +6,24 @@ from concourse.masks import make_identity
 BF16, F32, U16 = mybir.dt.bfloat16, mybir.dt.float32, mybir.dt.uint16
 ALU = mybir.AluOpType
 ACT = mybir.ActivationFunctionType
-AXIS_X = mybir.AxisListType.X
 
 P = 128
 B, T, C, H, DK, S, N = 2, 1024, 256, 2, 128, 4096, 2048
 SCALE = 32.0**-0.5
-BRANCHES = 2
+BR = 2
 CB = C // P
 KT = T // P
 BANK = 512
 IC = BANK
-IB = IC // P
-HALVES = T // BANK
-KH = KT // HALVES
-PIECE = 2
+QB = IC // P
+CHUNKS = T // IC
+VROW = DK + 2
+
+SUM_LAG = KT
+NORM_LAG = SUM_LAG + BR
+FLIP_LAG = NORM_LAG + 2
+ATT_LAG = FLIP_LAG + BR * (QB - 1) + 1
+OUT_LAG = ATT_LAG + 1
 
 FLOPS = 4 * 2 * C * C * N + 3 * B * H * 2 * DK * T * T
 
@@ -28,6 +32,7 @@ def tile_multiheadattention_b_kernel(
     tc, q, k, v, adj, adj1, attn_bias, edge_bias, wq, bq, wk, bk, wv, bv, wo, bo, base, offs, out
 ):
     nc = tc.nc
+    units = [(b, c, h) for b in range(B) for c in range(CHUNKS) for h in range(H)]
     with ExitStack() as ctx:
         held = ctx.enter_context(tc.tile_pool(name="held", bufs=1))
         work = ctx.enter_context(tc.tile_pool(name="work", bufs=2))
@@ -36,172 +41,246 @@ def tile_multiheadattention_b_kernel(
         offsets = held.tile([P, N // 16], U16, name="offsets")
         nc.sync.dma_start(offsets[:], offs)
 
+        staged = {}
+
+        def load_nodes(name, x_dram, b):
+            staged[name, b] = work.tile([P, CB, T], BF16, name=name + "_sb", bufs=1)
+            nc.sync.dma_start(staged[name, b][:], x_dram[:, b * T : (b + 1) * T].rearrange("(e p) n -> p e n", p=P))
+
+        mask_of = {}
+        adj1_of = {}
+        factor = {}
+
+        def load_unit(u):
+            b, c, h = units[u]
+            lo = c * IC
+            if h == 0:
+                mask_of[b, c] = work.tile([P, KT, BR, IC], BF16, name="masks")
+                nc.sync.dma_start(mask_of[b, c][:, :, 0, :], adj[b, :, lo : lo + IC].rearrange("(k p) i -> p k i", p=P))
+                adj1_of[b, c] = work.tile([P, KT, IC], BF16, name="adj1_sb")
+                nc.sync.dma_start(adj1_of[b, c][:], adj1[b, :, lo : lo + IC].rearrange("(k p) i -> p k i", p=P))
+            factor[u] = work.tile([P, KT, BR, IC], BF16, name="factor", bufs=3)
+            for br, bias_dram in enumerate((attn_bias, edge_bias)):
+                nc.sync.dma_start(
+                    factor[u][:, :, br, :], bias_dram[b, h, :, lo : lo + IC].rearrange("(k p) i -> p k i", p=P)
+                )
+
+        weights = {}
+
+        def load_weight(name, w_dram):
+            weights[name] = held.tile([P, CB, C], BF16, name=name)
+            nc.sync.dma_start(weights[name][:], w_dram.rearrange("(e p) c -> p e c", p=P))
+
+        load_weight("wk", wk)
+        load_nodes("k", k, 0)
+        load_weight("wq", wq)
+        load_nodes("q", q, 0)
+        load_unit(0)
+        load_weight("wv", wv)
+        load_nodes("v", v, 0)
+        load_unit(1)
+        load_weight("wo", wo)
+
+        bias_col = {}
+        for name, b_dram in (("bk", bk), ("bq", bq), ("bv", bv), ("bo", bo)):
+            bias_col[name] = held.tile([P, CB], F32, name=name + "_col")
+            nc.scalar.dma_start(bias_col[name][:], b_dram.rearrange("(a p) o -> p (a o)", p=P))
+
         ident_f32 = held.tile([P, P], F32, name="ident_f32")
         make_identity(nc, ident_f32[:])
         ident_bf16 = held.tile([P, P], BF16, name="ident_bf16")
         make_identity(nc, ident_bf16[:])
 
-        weights = {}
-        for name, w_dram in (("wk", wk), ("wq", wq), ("wv", wv), ("wo", wo)):
-            weights[name] = held.tile([P, CB, C], BF16, name=name)
-            nc.sync.dma_start(weights[name][:], w_dram.rearrange("(e p) c -> p e c", p=P))
-
-        bias_rows = held.tile([3 * CB, P], F32, name="bias_rows")
-        for j, b_dram in enumerate((bq, bk, bo)):
-            nc.sync.dma_start(bias_rows[j * CB : (j + 1) * CB, :], b_dram.rearrange("(e p) one -> e (p one)", p=P))
-        bias_ps = psum.tile([P, 3 * CB], F32, name="bias_ps", tag="acc", bufs=1)
-        nc.tensor.matmul(bias_ps[:], lhsT=bias_rows[:], rhs=ident_f32[0 : 3 * CB, 0 : 3 * CB], start=True, stop=True)
-        bias_cols = held.tile([P, 3 * CB], F32, name="bias_cols")
-        nc.vector.tensor_copy(bias_cols[:], bias_ps[:])
-        bv_all = held.tile([P, C], F32, name="bv_all")
-        nc.sync.dma_start(bv_all[:], bv.rearrange("c one -> (c one)").partition_broadcast(P))
-
-        y_sb = [held.tile([P, N], F32, name=f"y_sb{cb}") for cb in range(CB)]
         qh = held.tile([P, H, N], BF16, name="qh")
         kh = held.tile([P, H, N], BF16, name="kh")
-        vh_t = held.tile([P, B * KT, C], BF16, name="vh_t")
+        vh_ones = held.tile([P, B * KT, H, VROW], BF16, name="vh_ones")
+        nc.gpsimd.memset(vh_ones[:], 1.0)
+        y_sb = [held.tile([P, N], F32, name=f"y_sb{cb}") for cb in range(CB)]
+        bo_wide = [held.tile([P, N], F32, name=f"bo_wide{cb}") for cb in range(CB)]
+        for cb in range(CB):
+            nc.scalar.activation(bo_wide[cb][:], bias_col["bo"][:, cb : cb + 1].to_broadcast([P, N]), ACT.Copy)
 
-        for b in range(B):
-            staged = {}
-            for name, x_dram in (("k", k), ("q", q), ("v", v)):
-                staged[name] = work.tile([P, CB, T], BF16, name=name + "_sb", bufs=1)
-                nc.sync.dma_start(
-                    staged[name][:], x_dram[:, b * T : (b + 1) * T].rearrange("(e p) n -> p e n", p=P)
+        def project(dst, w_sb, x_sb, bias, h, n):
+            proj_ps = psum.tile([P, BANK], F32, name="proj_ps", tag="proj")
+            for e in range(CB):
+                nc.tensor.matmul(
+                    proj_ps[:],
+                    lhsT=w_sb[:, e, h * P : (h + 1) * P],
+                    rhs=x_sb[:, e, n * BANK : (n + 1) * BANK],
+                    start=(e == 0),
+                    stop=(e == CB - 1),
+                )
+            nc.scalar.activation(dst, proj_ps[:], ACT.Identity, bias=bias[:, h : h + 1])
+
+        qk_pieces = [(h, name, n) for h in range(H) for name in ("k", "q") for n in range(T // BANK)]
+
+        def project_qk(b, piece):
+            h, name, n = qk_pieces[piece]
+            dst = kh if name == "k" else qh
+            project(
+                dst[:, h, b * T + n * BANK : b * T + (n + 1) * BANK],
+                weights["w" + name], staged[name, b], bias_col["b" + name], h, n,
+            )
+
+        vh_of = {}
+        HALF = KT // 2
+
+        def project_v(b, piece):
+            h, n = divmod(piece % (H * 2), 2)
+            if piece == 0:
+                vh_of[b] = work.tile([P, H, T], BF16, name="vh_sb", bufs=1)
+            if piece < H * 2:
+                project(vh_of[b][:, h, n * BANK : (n + 1) * BANK], weights["wv"], staged["v", b], bias_col["bv"], h, n)
+            else:
+                turned_ps = psum.tile([P, HALF, P], BF16, name="turned_ps", tag="proj")
+                for j in range(HALF):
+                    kb = n * HALF + j
+                    nc.tensor.transpose(turned_ps[:, j, :], vh_of[b][:, h, kb * P : (kb + 1) * P], ident_bf16[:])
+                first = b * KT + n * HALF
+                nc.scalar.copy(vh_ones[:, first : first + HALF, h, 0:DK], turned_ps[:])
+
+        def mask_factors(u, kb):
+            b, c, h = units[u]
+            if h == 0:
+                nc.vector.tensor_tensor(
+                    mask_of[b, c][:, kb, 1, :], mask_of[b, c][:, kb, 0, :], adj1_of[b, c][:, kb, :], ALU.mult
+                )
+            nc.vector.tensor_tensor(factor[u][:, kb, :, :], factor[u][:, kb, :, :], mask_of[b, c][:, kb, :, :], ALU.mult)
+
+        expo = {}
+
+        def exponentials(u, kb):
+            b, c, h = units[u]
+            first_query = b * T + c * IC
+            if kb == 0:
+                expo[u] = work.tile([P, KT, BR, IC], BF16, name="expo")
+            raw_ps = psum.tile([P, IC], F32, name="raw_ps", bufs=3)
+            nc.tensor.matmul(
+                raw_ps[:],
+                lhsT=kh[:, h, b * T + kb * P : b * T + (kb + 1) * P],
+                rhs=qh[:, h, first_query : first_query + IC],
+                start=True,
+                stop=True,
+            )
+            logit = work.tile([P, BR, IC], F32, name="logit", bufs=4)
+            nc.vector.tensor_tensor(
+                logit[:], raw_ps[:].unsqueeze(1).to_broadcast([P, BR, IC]), factor[u][:, kb, :, :], ALU.mult
+            )
+            nc.scalar.activation(expo[u][:, kb, :, :], logit[:], ACT.Exp, scale=SCALE)
+
+        sums = {}
+
+        def weighted_sums(u, qb, br):
+            b, c, h = units[u]
+            if br == 0:
+                sums[u, qb] = psum.tile([P, BR, BANK // BR], F32, name="sums_ps")
+            for kb in range(KT):
+                nc.tensor.matmul(
+                    sums[u, qb][:, br, 0 : DK + 1],
+                    lhsT=expo[u][:, kb, br, qb * P : (qb + 1) * P],
+                    rhs=vh_ones[:, b * KT + kb, h, 0 : DK + 1],
+                    start=(kb == 0),
+                    stop=(kb == KT - 1),
                 )
 
-            for h in range(H):
-                for dst, w_sb, x_sb, first_col in ((kh, weights["wk"], staged["k"], CB), (qh, weights["wq"], staged["q"], 0)):
-                    for n in range(T // BANK):
-                        proj_ps = psum.tile([P, BANK], F32, name="proj_ps", tag="rows", bufs=3)
-                        for e in range(CB):
-                            nc.tensor.matmul(
-                                proj_ps[:],
-                                lhsT=w_sb[:, e, h * P : (h + 1) * P],
-                                rhs=x_sb[:, e, n * BANK : (n + 1) * BANK],
-                                start=(e == 0),
-                                stop=(e == CB - 1),
-                            )
-                        nc.scalar.activation(
-                            dst[:, h, b * T + n * BANK : b * T + (n + 1) * BANK],
-                            proj_ps[:],
-                            ACT.Identity,
-                            bias=bias_cols[:, first_col + h : first_col + h + 1],
-                        )
+        divided = {}
 
-            for kb in range(KT):
-                v_ps = psum.tile([P, C], F32, name="v_ps", tag="rows", bufs=3)
-                for e in range(CB):
-                    nc.tensor.matmul(
-                        v_ps[:],
-                        lhsT=staged["v"][:, e, kb * P : (kb + 1) * P],
-                        rhs=weights["wv"][:, e, :],
-                        start=(e == 0),
-                        stop=(e == CB - 1),
-                    )
-                nc.vector.tensor_tensor(vh_t[:, b * KT + kb, :], v_ps[:], bv_all[:], ALU.add)
+        def divide(u, qb):
+            recip = work.tile([P, BR, 1], F32, name="recip", bufs=4)
+            nc.vector.reciprocal(recip[:], sums[u, qb][:, :, DK : DK + 1])
+            divided[u, qb] = work.tile([P, BR, DK], F32, name="divided", bufs=4)
+            for br in range(BR):
+                nc.scalar.activation(
+                    divided[u, qb][:, br, :], sums[u, qb][:, br, 0:DK], ACT.Copy, scale=recip[:, br, :]
+                )
 
-            for lo in range(0, T, IC):
-                adj_sb = work.tile([P, KT, IC], BF16, name="adj_sb")
-                nc.sync.dma_start(adj_sb[:], adj[b, :, lo : lo + IC].rearrange("(k p) i -> p k i", p=P))
-                both_sb = work.tile([P, KT, IC], BF16, name="both_sb")
-                nc.sync.dma_start(both_sb[:], adj1[b, :, lo : lo + IC].rearrange("(k p) i -> p k i", p=P))
-                nc.vector.tensor_tensor(both_sb[:], both_sb[:], adj_sb[:], ALU.mult)
+        att_ps_of = {}
 
-                att = work.tile([P, H, IC], BF16, name="att")
+        def turn_and_add(u, qb):
+            if qb == 0:
+                att_ps_of[u] = psum.tile([P, IC], F32, name="att_ps", bufs=1)
+            for br in range(BR):
+                nc.tensor.matmul(
+                    att_ps_of[u][:, qb * P : (qb + 1) * P],
+                    lhsT=divided[u, qb][:, br, :],
+                    rhs=ident_f32[:],
+                    start=(br == 0),
+                    stop=(br == BR - 1),
+                )
+
+        att_of = {}
+
+        def round_att(u):
+            b, c, h = units[u]
+            if h == 0:
+                att_of[b, c] = work.tile([P, H, IC], BF16, name="att")
+            nc.scalar.copy(att_of[b, c][:, h, :], att_ps_of[u][:])
+
+        def project_out(b, c):
+            first_node = b * T + c * IC
+            for cb in range(CB):
+                y_ps = psum.tile([P, IC], F32, name="y_ps", tag="proj")
                 for h in range(H):
-                    factors = []
-                    for bias_dram in (attn_bias, edge_bias):
-                        factor = work.tile([P, KT, IC], BF16, name="factor", bufs=4)
-                        nc.sync.dma_start(
-                            factor[:], bias_dram[b, h, :, lo : lo + IC].rearrange("(k p) i -> p k i", p=P)
-                        )
-                        factors.append(factor)
-                    for k0 in range(0, KT, PIECE):
-                        for factor, mask_sb in zip(factors, (adj_sb, both_sb)):
-                            nc.gpsimd.tensor_tensor(
-                                factor[:, k0 : k0 + PIECE, :],
-                                factor[:, k0 : k0 + PIECE, :],
-                                mask_sb[:, k0 : k0 + PIECE, :],
-                                ALU.mult,
-                            )
+                    nc.tensor.matmul(
+                        y_ps[:],
+                        lhsT=weights["wo"][:, h, cb * P : (cb + 1) * P],
+                        rhs=att_of[b, c][:, h, :],
+                        start=(h == 0),
+                        stop=(h == H - 1),
+                    )
+                nc.scalar.copy(y_sb[cb][:, first_node : first_node + IC], y_ps[:])
 
-                    logits = [work.tile([P, KT, IC], F32, name="logits", bufs=4) for branch in range(BRANCHES)]
-                    for kb in range(KT):
-                        s_ps = psum.tile([P, IC], F32, name="s_ps", tag="raw")
-                        nc.tensor.matmul(
-                            s_ps[:],
-                            lhsT=kh[:, h, b * T + kb * P : b * T + (kb + 1) * P],
-                            rhs=qh[:, h, b * T + lo : b * T + lo + IC],
-                            start=True,
-                            stop=True,
-                        )
-                        for branch in range(BRANCHES):
-                            nc.vector.tensor_tensor(logits[branch][:, kb, :], s_ps[:], factors[branch][:, kb, :], ALU.mult)
+        window = []
 
-                    acc_ps = psum.tile([P, IC], F32, name="acc_ps", tag="acc", bufs=1)
-                    for branch in range(BRANCHES):
-                        probs = work.tile([P, KT, IC], BF16, name="probs", bufs=3)
-                        for ib in range(IB):
-                            rows_sb = work.tile([P, T], F32, name="rows_sb", bufs=4)
-                            half_max = work.tile([P, HALVES], F32, name="half_max", bufs=4)
-                            for half in range(HALVES):
-                                rows_ps = psum.tile([P, BANK], F32, name="rows_ps", tag="rows", bufs=3)
-                                for kk in range(KH):
-                                    nc.tensor.transpose(
-                                        rows_ps[:, kk * P : (kk + 1) * P],
-                                        logits[branch][:, half * KH + kk, ib * P : (ib + 1) * P],
-                                        ident_f32[:],
-                                    )
-                                nc.vector.tensor_scalar(
-                                    rows_sb[:, half * BANK : (half + 1) * BANK],
-                                    rows_ps[:],
-                                    SCALE,
-                                    None,
-                                    op0=ALU.mult,
-                                    op1=ALU.max,
-                                    accum_out=half_max[:, half : half + 1],
-                                )
-                            shift = work.tile([P, 1], F32, name="shift", bufs=4)
-                            nc.vector.reduce_max(shift[:], half_max[:], axis=AXIS_X, negate=True)
-                            expo_t = work.tile([P, T], BF16, name="expo_t", bufs=3)
-                            row_sum = work.tile([P, 1], F32, name="row_sum", bufs=4)
-                            nc.scalar.activation(expo_t[:], rows_sb[:], ACT.Exp, bias=shift[:], accum_out=row_sum[:])
-                            recip = work.tile([P, 1], F32, name="recip", bufs=4)
-                            nc.vector.reciprocal(recip[:], row_sum[:])
-                            diag = work.tile([P, P], BF16, name="diag", bufs=4)
-                            nc.scalar.activation(diag[:], ident_bf16[:], ACT.Copy, scale=recip[:])
-                            back_ps = psum.tile([P, KT, P], BF16, name="back_ps", tag="back")
-                            for kb in range(KT):
-                                nc.tensor.matmul(
-                                    back_ps[:, kb, :], lhsT=expo_t[:, kb * P : (kb + 1) * P], rhs=diag[:], start=True, stop=True
-                                )
-                            nc.scalar.copy(probs[:, :, ib * P : (ib + 1) * P], back_ps[:])
-                        for kb in range(KT):
-                            nc.tensor.matmul(
-                                acc_ps[:],
-                                lhsT=vh_t[:, b * KT + kb, h * DK : (h + 1) * DK],
-                                rhs=probs[:, kb, :],
-                                start=(branch == 0 and kb == 0),
-                                stop=(branch == BRANCHES - 1 and kb == KT - 1),
-                            )
-                    nc.scalar.activation(att[:, h, :], acc_ps[:], ACT.Copy)
+        def turn_of(step, lag):
+            u, i = divmod(step - lag, KT)
+            return (u, i) if 0 <= u < len(units) else None
 
-                for cb in range(CB):
-                    y_ps = psum.tile([P, IC], F32, name="y_ps", tag="acc", bufs=1)
-                    for h in range(H):
-                        nc.tensor.matmul(
-                            y_ps[:],
-                            lhsT=weights["wo"][:, h, cb * P : (cb + 1) * P],
-                            rhs=att[:, h, :],
-                            start=(h == 0),
-                            stop=(h == H - 1),
-                        )
-                    nc.scalar.activation(y_sb[cb][:, b * T + lo : b * T + lo + IC], y_ps[:], ACT.Copy)
+        for piece in range(len(qk_pieces)):
+            project_qk(0, piece)
+        for kb in range(KT):
+            mask_factors(0, kb)
+
+        for step in range(KT * len(units) + OUT_LAG + 1):
+            now = turn_of(step, 0)
+            if now:
+                u, kb = now
+                b, c, h = units[u]
+                if kb == 0 and u + 2 < len(units):
+                    load_unit(u + 2)
+                if kb == 0 and u + 2 >= len(units):
+                    cb = u + 2 - len(units)
+                    window.append(work.tile([P, S], F32, name="window", tag="factor", bufs=3))
+                    nc.sync.dma_start(window[cb][:], base[cb * P : (cb + 1) * P, :])
+                if kb == 0 and u == 1:
+                    for name, x_dram in (("k", k), ("q", q), ("v", v)):
+                        load_nodes(name, x_dram, 1)
+                exponentials(u, kb)
+
+            summing = turn_of(step, SUM_LAG)
+            if summing:
+                weighted_sums(summing[0], summing[1] // BR, summing[1] % BR)
+            dividing = turn_of(step, NORM_LAG)
+            if dividing and dividing[1] % BR == 0:
+                divide(dividing[0], dividing[1] // BR)
+            turning = turn_of(step, FLIP_LAG)
+            if turning and turning[1] % BR == 0:
+                turn_and_add(turning[0], turning[1] // BR)
+            rounding = turn_of(step, ATT_LAG)
+            if rounding and rounding[1] == 0:
+                round_att(rounding[0])
+            leaving = turn_of(step, OUT_LAG)
+            if leaving and leaving[1] == 0 and units[leaving[0]][2] == H - 1:
+                project_out(units[leaving[0]][0], units[leaving[0]][1])
+
+            if now:
+                if u + 1 < len(units):
+                    mask_factors(u + 1, kb)
+                if (c, h) == (0, 0):
+                    project_v(b, kb)
+                if (c, h) == (CHUNKS - 1, H - 1) and b + 1 < B:
+                    project_qk(b + 1, kb)
 
         for cb in range(CB):
-            window = work.tile([P, S], F32, name="window", tag="logits", bufs=4)
-            nc.sync.dma_start(window[:], base[cb * P : (cb + 1) * P, :])
-            bo_wide = work.tile([P, N], F32, name="bo_wide", tag="factor", bufs=4)
-            nc.scalar.activation(bo_wide[:], bias_cols[:, 2 * CB + cb : 2 * CB + cb + 1].to_broadcast([P, N]), ACT.Copy)
-            nc.vector.tensor_tensor(window[:].indirect(offsets[:]), y_sb[cb][:], bo_wide[:], ALU.add)
-            nc.sync.dma_start(out[cb * P : (cb + 1) * P, :], window[:])
+            nc.vector.tensor_tensor(window[cb][:].indirect(offsets[:]), y_sb[cb][:], bo_wide[cb][:], ALU.add)
+            nc.sync.dma_start(out[cb * P : (cb + 1) * P, :], window[cb][:])

@@ -24,6 +24,11 @@ NORM_LAG = SUM_LAG + BR
 FLIP_LAG = NORM_LAG + 2
 ATT_LAG = FLIP_LAG + BR * (QB - 1) + 1
 OUT_LAG = ATT_LAG + 1
+STEPS_OF_GRAPH = CHUNKS * H * KT
+V_PIECES = 4 * H
+V_LAG = SUM_LAG - V_PIECES // H
+FIRST_BLOCKS = 2
+MASK_LEAD = 2
 
 FLOPS = 4 * 2 * C * C * N + 3 * B * H * 2 * DK * T * T
 
@@ -51,19 +56,31 @@ def tile_multiheadattention_b_kernel(
         adj1_of = {}
         factor = {}
 
-        def load_unit(u):
+        def load_unit(u, blocks):
             b, c, h = units[u]
             lo = c * IC
             if h == 0:
                 mask_of[b, c] = work.tile([P, KT, BR, IC], BF16, name="masks")
-                nc.sync.dma_start(mask_of[b, c][:, :, 0, :], adj[b, :, lo : lo + IC].rearrange("(k p) i -> p k i", p=P))
                 adj1_of[b, c] = work.tile([P, KT, IC], BF16, name="adj1_sb")
-                nc.sync.dma_start(adj1_of[b, c][:], adj1[b, :, lo : lo + IC].rearrange("(k p) i -> p k i", p=P))
             factor[u] = work.tile([P, KT, BR, IC], BF16, name="factor", bufs=3)
-            for br, bias_dram in enumerate((attn_bias, edge_bias)):
-                nc.sync.dma_start(
-                    factor[u][:, :, br, :], bias_dram[b, h, :, lo : lo + IC].rearrange("(k p) i -> p k i", p=P)
-                )
+            for k0 in range(0, KT, blocks):
+                keys = slice(k0 * P, (k0 + blocks) * P)
+                pairs = [
+                    (factor[u][:, k0 : k0 + blocks, 0, :], attn_bias[b, h, keys, lo : lo + IC]),
+                    (factor[u][:, k0 : k0 + blocks, 1, :], edge_bias[b, h, keys, lo : lo + IC]),
+                ]
+                if h == 0:
+                    pairs = [
+                        (mask_of[b, c][:, k0 : k0 + blocks, 0, :], adj[b, keys, lo : lo + IC]),
+                        (adj1_of[b, c][:, k0 : k0 + blocks, :], adj1[b, keys, lo : lo + IC]),
+                    ] + pairs
+                for tile_part, dram_part in pairs:
+                    nc.sync.dma_start(tile_part, dram_part.rearrange("(k p) i -> p k i", p=P))
+            if h == 0:
+                for kb in range(KT):
+                    nc.gpsimd.tensor_tensor(
+                        mask_of[b, c][:, kb, 1, :], mask_of[b, c][:, kb, 0, :], adj1_of[b, c][:, kb, :], ALU.mult
+                    )
 
         weights = {}
 
@@ -75,10 +92,10 @@ def tile_multiheadattention_b_kernel(
         load_nodes("k", k, 0)
         load_weight("wq", wq)
         load_nodes("q", q, 0)
-        load_unit(0)
+        load_unit(0, FIRST_BLOCKS)
         load_weight("wv", wv)
         load_nodes("v", v, 0)
-        load_unit(1)
+        load_unit(1, KT)
         load_weight("wo", wo)
 
         bias_col = {}
@@ -97,8 +114,6 @@ def tile_multiheadattention_b_kernel(
         nc.gpsimd.memset(vh_ones[:], 1.0)
         y_sb = [held.tile([P, N], F32, name=f"y_sb{cb}") for cb in range(CB)]
         bo_wide = [held.tile([P, N], F32, name=f"bo_wide{cb}") for cb in range(CB)]
-        for cb in range(CB):
-            nc.scalar.activation(bo_wide[cb][:], bias_col["bo"][:, cb : cb + 1].to_broadcast([P, N]), ACT.Copy)
 
         def project(dst, w_sb, x_sb, bias, h, n):
             proj_ps = psum.tile([P, BANK], F32, name="proj_ps", tag="proj")
@@ -126,10 +141,11 @@ def tile_multiheadattention_b_kernel(
         HALF = KT // 2
 
         def project_v(b, piece):
-            h, n = divmod(piece % (H * 2), 2)
+            h, part = divmod(piece, 4)
+            n = part % 2
             if piece == 0:
                 vh_of[b] = work.tile([P, H, T], BF16, name="vh_sb", bufs=1)
-            if piece < H * 2:
+            if part < 2:
                 project(vh_of[b][:, h, n * BANK : (n + 1) * BANK], weights["wv"], staged["v", b], bias_col["bv"], h, n)
             else:
                 turned_ps = psum.tile([P, HALF, P], BF16, name="turned_ps", tag="proj")
@@ -141,10 +157,6 @@ def tile_multiheadattention_b_kernel(
 
         def mask_factors(u, kb):
             b, c, h = units[u]
-            if h == 0:
-                nc.vector.tensor_tensor(
-                    mask_of[b, c][:, kb, 1, :], mask_of[b, c][:, kb, 0, :], adj1_of[b, c][:, kb, :], ALU.mult
-                )
             nc.vector.tensor_tensor(factor[u][:, kb, :, :], factor[u][:, kb, :, :], mask_of[b, c][:, kb, :, :], ALU.mult)
 
         expo = {}
@@ -238,23 +250,24 @@ def tile_multiheadattention_b_kernel(
 
         for piece in range(len(qk_pieces)):
             project_qk(0, piece)
-        for kb in range(KT):
-            mask_factors(0, kb)
 
-        for step in range(KT * len(units) + OUT_LAG + 1):
+        for step in range(-MASK_LEAD, KT * len(units) + OUT_LAG + 1):
             now = turn_of(step, 0)
             if now:
                 u, kb = now
                 b, c, h = units[u]
                 if kb == 0 and u + 2 < len(units):
-                    load_unit(u + 2)
+                    load_unit(u + 2, KT)
                 if kb == 0 and u + 2 >= len(units):
                     cb = u + 2 - len(units)
                     window.append(work.tile([P, S], F32, name="window", tag="factor", bufs=3))
                     nc.sync.dma_start(window[cb][:], base[cb * P : (cb + 1) * P, :])
-                if kb == 0 and u == 1:
+                if kb == 0 and u == 2:
                     for name, x_dram in (("k", k), ("q", q), ("v", v)):
                         load_nodes(name, x_dram, 1)
+                if kb == 0 and 1 <= u <= CB:
+                    cb = u - 1
+                    nc.scalar.activation(bo_wide[cb][:], bias_col["bo"][:, cb : cb + 1].to_broadcast([P, N]), ACT.Copy)
                 exponentials(u, kb)
 
             summing = turn_of(step, SUM_LAG)
@@ -273,13 +286,16 @@ def tile_multiheadattention_b_kernel(
             if leaving and leaving[1] == 0 and units[leaving[0]][2] == H - 1:
                 project_out(units[leaving[0]][0], units[leaving[0]][1])
 
+            masking = turn_of(step, -MASK_LEAD)
+            if masking:
+                mask_factors(masking[0], masking[1])
+
             if now:
-                if u + 1 < len(units):
-                    mask_factors(u + 1, kb)
-                if (c, h) == (0, 0):
-                    project_v(b, kb)
                 if (c, h) == (CHUNKS - 1, H - 1) and b + 1 < B:
                     project_qk(b + 1, kb)
+                v_piece = step - b * STEPS_OF_GRAPH - V_LAG
+                if 0 <= v_piece < V_PIECES:
+                    project_v(b, v_piece)
 
         for cb in range(CB):
             nc.vector.tensor_tensor(window[cb][:].indirect(offsets[:]), y_sb[cb][:], bo_wide[cb][:], ALU.add)

@@ -218,6 +218,7 @@ def tile_multiheadattention_b_kernel(
                     rhs=ident_f32[:],
                     start=(br == 0),
                     stop=(br == BR - 1),
+                    is_transpose=True,
                 )
 
         att_of = {}

@@ -25,8 +25,9 @@ FLIP_LAG = NORM_LAG + 2
 ATT_LAG = FLIP_LAG + BR * (QB - 1) + 1
 OUT_LAG = ATT_LAG + 1
 STEPS_OF_GRAPH = CHUNKS * H * KT
-V_PIECES = 4 * H
-V_LAG = SUM_LAG - V_PIECES // H
+V_BLOCKS = 2
+V_PIECES = KT // V_BLOCKS
+V_LAG = SUM_LAG - V_PIECES
 FIRST_BLOCKS = 2
 MASK_LEAD = 2
 
@@ -99,14 +100,18 @@ def tile_multiheadattention_b_kernel(
         load_weight("wo", wo)
 
         bias_col = {}
-        for name, b_dram in (("bk", bk), ("bq", bq), ("bv", bv), ("bo", bo)):
+        for name, b_dram in (("bk", bk), ("bq", bq), ("bo", bo)):
             bias_col[name] = held.tile([P, CB], F32, name=name + "_col")
             nc.scalar.dma_start(bias_col[name][:], b_dram.rearrange("(a p) o -> p (a o)", p=P))
 
         ident_f32 = held.tile([P, P], F32, name="ident_f32")
         make_identity(nc, ident_f32[:])
-        ident_bf16 = held.tile([P, P], BF16, name="ident_bf16")
-        make_identity(nc, ident_bf16[:])
+        ones_row = held.tile([P, P], F32, name="ones_row")
+        nc.vector.memset(ones_row[:], 0.0)
+        nc.vector.memset(ones_row[0:1, :], 1.0)
+        bv_row = held.tile([P, C], F32, name="bv_row")
+        nc.vector.memset(bv_row[:], 0.0)
+        nc.scalar.dma_start(bv_row[0:1, :], bv.rearrange("c o -> o c"))
 
         qh = held.tile([P, H, N], BF16, name="qh")
         kh = held.tile([P, H, N], BF16, name="kh")
@@ -137,23 +142,23 @@ def tile_multiheadattention_b_kernel(
                 weights["w" + name], staged[name, b], bias_col["b" + name], h, n,
             )
 
-        vh_of = {}
-        HALF = KT // 2
-
         def project_v(b, piece):
-            h, part = divmod(piece, 4)
-            n = part % 2
-            if piece == 0:
-                vh_of[b] = work.tile([P, H, T], BF16, name="vh_sb", bufs=1)
-            if part < 2:
-                project(vh_of[b][:, h, n * BANK : (n + 1) * BANK], weights["wv"], staged["v", b], bias_col["bv"], h, n)
-            else:
-                turned_ps = psum.tile([P, HALF, P], BF16, name="turned_ps", tag="proj")
-                for j in range(HALF):
-                    kb = n * HALF + j
-                    nc.tensor.transpose(turned_ps[:, j, :], vh_of[b][:, h, kb * P : (kb + 1) * P], ident_bf16[:])
-                first = b * KT + n * HALF
-                nc.scalar.copy(vh_ones[:, first : first + HALF, h, 0:DK], turned_ps[:])
+            v_ps = psum.tile([P, V_BLOCKS, C], F32, name="v_ps", tag="proj")
+            for j in range(V_BLOCKS):
+                kb = piece * V_BLOCKS + j
+                for e in range(CB):
+                    nc.tensor.matmul(
+                        v_ps[:, j, :],
+                        lhsT=staged["v", b][:, e, kb * P : (kb + 1) * P],
+                        rhs=weights["wv"][:, e, :],
+                        start=(e == 0),
+                        stop=False,
+                    )
+                nc.tensor.matmul(v_ps[:, j, :], lhsT=ones_row[:], rhs=bv_row[:], start=False, stop=True)
+            first = b * KT + piece * V_BLOCKS
+            nc.scalar.copy(
+                vh_ones[:, first : first + V_BLOCKS, :, 0:DK], v_ps[:].rearrange("p j (h d) -> p j h d", h=H)
+            )
 
         def mask_factors(u, kb):
             b, c, h = units[u]

@@ -78,8 +78,9 @@ def tile_multiheadattention_b_kernel(
                 for tile_part, dram_part in pairs:
                     nc.sync.dma_start(tile_part, dram_part.rearrange("(k p) i -> p k i", p=P))
             if h == 0:
+                engine = nc.vector if u == 0 else nc.gpsimd
                 for kb in range(KT):
-                    nc.gpsimd.tensor_tensor(
+                    engine.tensor_tensor(
                         mask_of[b, c][:, kb, 1, :], mask_of[b, c][:, kb, 0, :], adj1_of[b, c][:, kb, :], ALU.mult
                     )
 

@@ -28,7 +28,7 @@ STEPS_OF_GRAPH = CHUNKS * H * KT
 V_BLOCKS = 2
 V_PIECES = KT // V_BLOCKS
 V_LAG = SUM_LAG - V_PIECES
-FIRST_BLOCKS = 2
+FIRST_BLOCKS = 4
 MASK_LEAD = 2
 
 FLOPS = 4 * 2 * C * C * N + 3 * B * H * 2 * DK * T * T

@@ -28,7 +28,9 @@ STEPS_OF_GRAPH = CHUNKS * H * KT
 V_BLOCKS = 2
 V_PIECES = KT // V_BLOCKS
 V_LAG = SUM_LAG - V_PIECES
-FIRST_BLOCKS = 4
+FIRST_BLOCKS = 2
+NEXT_BLOCKS = 4
+PIECE_LEAD = 3
 MASK_LEAD = 2
 
 FLOPS = 4 * 2 * C * C * N + 3 * B * H * 2 * DK * T * T
@@ -49,61 +51,73 @@ def tile_multiheadattention_b_kernel(
 
         staged = {}
 
-        def load_nodes(name, x_dram, b):
-            staged[name, b] = work.tile([P, CB, T], BF16, name=name + "_sb", bufs=1)
-            nc.sync.dma_start(staged[name, b][:], x_dram[:, b * T : (b + 1) * T].rearrange("(e p) n -> p e n", p=P))
+        def load_nodes(queue, name, x_dram, b, first, count):
+            if first == 0:
+                staged[name, b] = work.tile([P, CB, T], BF16, name=name + "_sb", bufs=1)
+            queue.dma_start(
+                staged[name, b][:, :, first : first + count],
+                x_dram[:, b * T + first : b * T + first + count].rearrange("(e p) n -> p e n", p=P),
+            )
 
         mask_of = {}
         adj1_of = {}
         factor = {}
 
-        def load_unit(u, blocks):
+        def load_blocks(u, k0, blocks):
             b, c, h = units[u]
             lo = c * IC
-            if h == 0:
+            if k0 == 0 and h == 0:
                 mask_of[b, c] = work.tile([P, KT, BR, IC], BF16, name="masks")
                 adj1_of[b, c] = work.tile([P, KT, IC], BF16, name="adj1_sb")
-            factor[u] = work.tile([P, KT, BR, IC], BF16, name="factor", bufs=3)
-            for k0 in range(0, KT, blocks):
-                keys = slice(k0 * P, (k0 + blocks) * P)
+            if k0 == 0:
+                factor[u] = work.tile([P, KT, BR, IC], BF16, name="factor", bufs=3)
+            keys = slice(k0 * P, (k0 + blocks) * P)
+            pairs = [
+                (factor[u][:, k0 : k0 + blocks, 0, :], attn_bias[b, h, keys, lo : lo + IC]),
+                (factor[u][:, k0 : k0 + blocks, 1, :], edge_bias[b, h, keys, lo : lo + IC]),
+            ]
+            if h == 0:
                 pairs = [
-                    (factor[u][:, k0 : k0 + blocks, 0, :], attn_bias[b, h, keys, lo : lo + IC]),
-                    (factor[u][:, k0 : k0 + blocks, 1, :], edge_bias[b, h, keys, lo : lo + IC]),
-                ]
-                if h == 0:
-                    pairs = [
-                        (mask_of[b, c][:, k0 : k0 + blocks, 0, :], adj[b, keys, lo : lo + IC]),
-                        (adj1_of[b, c][:, k0 : k0 + blocks, :], adj1[b, keys, lo : lo + IC]),
-                    ] + pairs
-                for tile_part, dram_part in pairs:
-                    nc.sync.dma_start(tile_part, dram_part.rearrange("(k p) i -> p k i", p=P))
+                    (mask_of[b, c][:, k0 : k0 + blocks, 0, :], adj[b, keys, lo : lo + IC]),
+                    (adj1_of[b, c][:, k0 : k0 + blocks, :], adj1[b, keys, lo : lo + IC]),
+                ] + pairs
+            for tile_part, dram_part in pairs:
+                nc.sync.dma_start(tile_part, dram_part.rearrange("(k p) i -> p k i", p=P))
             if h == 0:
                 engine = nc.vector if u == 0 else nc.gpsimd
-                for kb in range(KT):
+                for kb in range(k0, k0 + blocks):
                     engine.tensor_tensor(
                         mask_of[b, c][:, kb, 1, :], mask_of[b, c][:, kb, 0, :], adj1_of[b, c][:, kb, :], ALU.mult
                     )
 
+        def load_unit(u, blocks):
+            for k0 in range(0, KT, blocks):
+                load_blocks(u, k0, blocks)
+
         weights = {}
 
-        def load_weight(name, w_dram):
+        def load_weight(queue, name, w_dram):
             weights[name] = held.tile([P, CB, C], BF16, name=name)
-            nc.sync.dma_start(weights[name][:], w_dram.rearrange("(e p) c -> p e c", p=P))
-
-        load_weight("wk", wk)
-        load_nodes("k", k, 0)
-        load_weight("wq", wq)
-        load_nodes("q", q, 0)
-        load_unit(0, FIRST_BLOCKS)
-        load_weight("wv", wv)
-        load_nodes("v", v, 0)
-        load_unit(1, KT)
-        load_weight("wo", wo)
+            queue.dma_start(weights[name][:], w_dram.rearrange("(e p) c -> p e c", p=P))
 
         bias_col = {}
-        for name, b_dram in (("bk", bk), ("bq", bq), ("bo", bo)):
+
+        def load_bias(name, b_dram):
             bias_col[name] = held.tile([P, CB], F32, name=name + "_col")
-            nc.scalar.dma_start(bias_col[name][:], b_dram.rearrange("(a p) o -> p (a o)", p=P))
+            nc.sync.dma_start(bias_col[name][:], b_dram.rearrange("(a p) o -> p (a o)", p=P))
+
+        load_weight(nc.scalar, "wk", wk)
+        load_nodes(nc.scalar, "k", k, 0, 0, T)
+        load_weight(nc.scalar, "wq", wq)
+        load_nodes(nc.scalar, "q", q, 0, 0, IC)
+        load_bias("bk", bk)
+        load_bias("bq", bq)
+        load_bias("bo", bo)
+        load_blocks(0, 0, FIRST_BLOCKS)
+        load_blocks(0, FIRST_BLOCKS, FIRST_BLOCKS)
+        load_blocks(0, 2 * FIRST_BLOCKS, FIRST_BLOCKS)
+        load_weight(nc.sync, "wv", wv)
+        load_nodes(nc.sync, "v", v, 0, 0, T)
 
         ident_f32 = held.tile([P, P], F32, name="ident_f32")
         make_identity(nc, ident_f32[:])
@@ -112,7 +126,11 @@ def tile_multiheadattention_b_kernel(
         nc.vector.memset(ones_row[0:1, :], 1.0)
         bv_row = held.tile([P, C], F32, name="bv_row")
         nc.vector.memset(bv_row[:], 0.0)
-        nc.scalar.dma_start(bv_row[0:1, :], bv.rearrange("c o -> o c"))
+        nc.sync.dma_start(bv_row[0:1, :], bv.rearrange("c o -> o c"))
+        load_blocks(0, 3 * FIRST_BLOCKS, FIRST_BLOCKS)
+        load_unit(1, NEXT_BLOCKS)
+        load_nodes(nc.sync, "q", q, 0, IC, T - IC)
+        load_weight(nc.sync, "wo", wo)
 
         qh = held.tile([P, H, N], BF16, name="qh")
         kh = held.tile([P, H, N], BF16, name="kh")
@@ -120,8 +138,10 @@ def tile_multiheadattention_b_kernel(
         nc.gpsimd.memset(vh_ones[:], 1.0)
         y_sb = [held.tile([P, N], F32, name=f"y_sb{cb}") for cb in range(CB)]
         bo_wide = [held.tile([P, N], F32, name=f"bo_wide{cb}") for cb in range(CB)]
+        for cb in range(CB):
+            nc.scalar.activation(bo_wide[cb][:], bias_col["bo"][:, cb : cb + 1].to_broadcast([P, N]), ACT.Copy)
 
-        def project(dst, w_sb, x_sb, bias, h, n):
+        def project(dst, w_sb, x_sb, bias, h, n, by_vector):
             proj_ps = psum.tile([P, BANK], F32, name="proj_ps", tag="proj")
             for e in range(CB):
                 nc.tensor.matmul(
@@ -131,17 +151,20 @@ def tile_multiheadattention_b_kernel(
                     start=(e == 0),
                     stop=(e == CB - 1),
                 )
-            nc.scalar.activation(dst, proj_ps[:], ACT.Identity, bias=bias[:, h : h + 1])
+            if by_vector:
+                nc.vector.tensor_scalar_add(dst, proj_ps[:], bias[:, h : h + 1])
+            else:
+                nc.scalar.activation(dst, proj_ps[:], ACT.Identity, bias=bias[:, h : h + 1])
 
-        qk_pieces = [(h, name, n) for h in range(H) for name in ("k", "q") for n in range(T // BANK)]
-
-        def project_qk(b, piece):
-            h, name, n = qk_pieces[piece]
+        def project_qk(b, name, h, n, by_vector):
             dst = kh if name == "k" else qh
             project(
                 dst[:, h, b * T + n * BANK : b * T + (n + 1) * BANK],
-                weights["w" + name], staged[name, b], bias_col["b" + name], h, n,
+                weights["w" + name], staged[name, b], bias_col["b" + name], h, n, by_vector,
             )
+
+        qk_pieces = [("k", h, n, h * KT + n * (BANK // P)) for h in range(H) for n in range(T // BANK)]
+        qk_pieces += [("q", h, n, (n * H + h) * KT) for h in range(H) for n in range(T // BANK)]
 
         def project_v(b, piece):
             v_ps = psum.tile([P, V_BLOCKS, C], F32, name="v_ps", tag="proj")
@@ -255,26 +278,26 @@ def tile_multiheadattention_b_kernel(
             u, i = divmod(step - lag, KT)
             return (u, i) if 0 <= u < len(units) else None
 
-        for piece in range(len(qk_pieces)):
-            project_qk(0, piece)
+        for step in range(-PIECE_LEAD, KT * len(units) + OUT_LAG + 1):
+            for b in range(B):
+                for name, h, n, first_use in qk_pieces:
+                    if step == b * STEPS_OF_GRAPH + first_use - PIECE_LEAD:
+                        project_qk(b, name, h, n, by_vector=step < 0)
 
-        for step in range(-MASK_LEAD, KT * len(units) + OUT_LAG + 1):
             now = turn_of(step, 0)
             if now:
                 u, kb = now
                 b, c, h = units[u]
-                if kb == 0 and u + 2 < len(units):
-                    load_unit(u + 2, KT)
+
                 if kb == 0 and u + 2 >= len(units):
                     cb = u + 2 - len(units)
                     window.append(work.tile([P, S], F32, name="window", tag="factor", bufs=3))
                     nc.sync.dma_start(window[cb][:], base[cb * P : (cb + 1) * P, :])
-                if kb == 0 and u == 2:
+                if kb == 0 and u == len(units) // B - 1:
                     for name, x_dram in (("k", k), ("q", q), ("v", v)):
-                        load_nodes(name, x_dram, 1)
-                if kb == 0 and 1 <= u <= CB:
-                    cb = u - 1
-                    nc.scalar.activation(bo_wide[cb][:], bias_col["bo"][:, cb : cb + 1].to_broadcast([P, N]), ACT.Copy)
+                        load_nodes(nc.sync, name, x_dram, 1, 0, T)
+                if kb == 0 and u + 2 < len(units):
+                    load_unit(u + 2, NEXT_BLOCKS if u == 0 else KT)
                 exponentials(u, kb)
 
             summing = turn_of(step, SUM_LAG)
@@ -298,8 +321,6 @@ def tile_multiheadattention_b_kernel(
                 mask_factors(masking[0], masking[1])
 
             if now:
-                if (c, h) == (CHUNKS - 1, H - 1) and b + 1 < B:
-                    project_qk(b + 1, kb)
                 v_piece = step - b * STEPS_OF_GRAPH - V_LAG
                 if 0 <= v_piece < V_PIECES:
                     project_v(b, v_piece)

@@ -41,13 +41,14 @@ def tile_multiheadattention_b_kernel(
 ):
     nc = tc.nc
     units = [(b, c, h) for b in range(B) for c in range(CHUNKS) for h in range(H)]
+    passes = [(u, 0, IC) for u in range(len(units) - 1)]
+    passes += [(len(units) - 1, 0, IC // 2), (len(units) - 1, IC // 2, IC // 2)]
     with ExitStack() as ctx:
         held = ctx.enter_context(tc.tile_pool(name="held", bufs=1))
         work = ctx.enter_context(tc.tile_pool(name="work", bufs=2))
         psum = ctx.enter_context(tc.psum_pool(name="psum", bufs=2))
 
         offsets = held.tile([P, N // 16], U16, name="offsets")
-        nc.sync.dma_start(offsets[:], offs)
 
         staged = {}
 
@@ -83,12 +84,15 @@ def tile_multiheadattention_b_kernel(
                 ] + pairs
             for tile_part, dram_part in pairs:
                 nc.sync.dma_start(tile_part, dram_part.rearrange("(k p) i -> p k i", p=P))
-            if h == 0:
-                engine = nc.vector if u == 0 else nc.gpsimd
+            if h == 0 and u > 0:
                 for kb in range(k0, k0 + blocks):
-                    engine.tensor_tensor(
-                        mask_of[b, c][:, kb, 1, :], mask_of[b, c][:, kb, 0, :], adj1_of[b, c][:, kb, :], ALU.mult
-                    )
+                    local_mask(nc.gpsimd, u, kb)
+
+        def local_mask(engine, u, kb):
+            b, c, h = units[u]
+            engine.tensor_tensor(
+                mask_of[b, c][:, kb, 1, :], mask_of[b, c][:, kb, 0, :], adj1_of[b, c][:, kb, :], ALU.mult
+            )
 
         def load_unit(u, blocks):
             for k0 in range(0, KT, blocks):
@@ -102,18 +106,18 @@ def tile_multiheadattention_b_kernel(
 
         bias_col = {}
 
-        def load_bias(name, b_dram):
+        def load_bias(queue, name, b_dram):
             bias_col[name] = held.tile([P, CB], F32, name=name + "_col")
-            nc.sync.dma_start(bias_col[name][:], b_dram.rearrange("(a p) o -> p (a o)", p=P))
+            queue.dma_start(bias_col[name][:], b_dram.rearrange("(a p) o -> p (a o)", p=P))
 
         load_weight(nc.scalar, "wk", wk)
         load_nodes(nc.scalar, "k", k, 0, 0, T)
+        load_bias(nc.scalar, "bk", bk)
         load_weight(nc.scalar, "wq", wq)
         load_nodes(nc.scalar, "q", q, 0, 0, IC)
-        load_bias("bk", bk)
-        load_bias("bq", bq)
-        load_bias("bo", bo)
+        load_bias(nc.scalar, "bq", bq)
         load_blocks(0, 0, FIRST_BLOCKS)
+        load_bias(nc.sync, "bo", bo)
         load_blocks(0, FIRST_BLOCKS, FIRST_BLOCKS)
         load_blocks(0, 2 * FIRST_BLOCKS, FIRST_BLOCKS)
         load_weight(nc.sync, "wv", wv)
@@ -131,6 +135,7 @@ def tile_multiheadattention_b_kernel(
         load_unit(1, NEXT_BLOCKS)
         load_nodes(nc.sync, "q", q, 0, IC, T - IC)
         load_weight(nc.sync, "wo", wo)
+        nc.sync.dma_start(offsets[:], offs)
 
         qh = held.tile([P, H, N], BF16, name="qh")
         kh = held.tile([P, H, N], BF16, name="kh")
@@ -190,35 +195,39 @@ def tile_multiheadattention_b_kernel(
 
         expo = {}
 
-        def exponentials(u, kb):
+        def exponentials(p, kb):
+            u, lo, width = passes[p]
             b, c, h = units[u]
-            first_query = b * T + c * IC
+            first_query = b * T + c * IC + lo
             if kb == 0:
-                expo[u] = work.tile([P, KT, BR, IC], BF16, name="expo")
-            raw_ps = psum.tile([P, IC], F32, name="raw_ps", bufs=3)
+                expo[p] = work.tile([P, KT, BR, width], BF16, name="expo")
+            raw_ps = psum.tile([P, width], F32, name="raw_ps", bufs=3)
             nc.tensor.matmul(
                 raw_ps[:],
                 lhsT=kh[:, h, b * T + kb * P : b * T + (kb + 1) * P],
-                rhs=qh[:, h, first_query : first_query + IC],
+                rhs=qh[:, h, first_query : first_query + width],
                 start=True,
                 stop=True,
             )
-            logit = work.tile([P, BR, IC], F32, name="logit", bufs=4)
+            logit = work.tile([P, BR, width], F32, name="logit", bufs=4)
             nc.vector.tensor_tensor(
-                logit[:], raw_ps[:].unsqueeze(1).to_broadcast([P, BR, IC]), factor[u][:, kb, :, :], ALU.mult
+                logit[:],
+                raw_ps[:].unsqueeze(1).to_broadcast([P, BR, width]),
+                factor[u][:, kb, :, lo : lo + width],
+                ALU.mult,
             )
-            nc.scalar.activation(expo[u][:, kb, :, :], logit[:], ACT.Exp, scale=SCALE)
+            nc.scalar.activation(expo[p][:, kb, :, :], logit[:], ACT.Exp, scale=SCALE)
 
         sums = {}
 
-        def weighted_sums(u, qb, br):
-            b, c, h = units[u]
+        def weighted_sums(p, qb, br):
+            b, c, h = units[passes[p][0]]
             if br == 0:
-                sums[u, qb] = psum.tile([P, BR, BANK // BR], F32, name="sums_ps")
+                sums[p, qb] = psum.tile([P, BR, BANK // BR], F32, name="sums_ps")
             for kb in range(KT):
                 nc.tensor.matmul(
-                    sums[u, qb][:, br, 0 : DK + 1],
-                    lhsT=expo[u][:, kb, br, qb * P : (qb + 1) * P],
+                    sums[p, qb][:, br, 0 : DK + 1],
+                    lhsT=expo[p][:, kb, br, qb * P : (qb + 1) * P],
                     rhs=vh_ones[:, b * KT + kb, h, 0 : DK + 1],
                     start=(kb == 0),
                     stop=(kb == KT - 1),
@@ -226,24 +235,24 @@ def tile_multiheadattention_b_kernel(
 
         divided = {}
 
-        def divide(u, qb):
+        def divide(p, qb):
             recip = work.tile([P, BR, 1], F32, name="recip", bufs=4)
-            nc.vector.reciprocal(recip[:], sums[u, qb][:, :, DK : DK + 1])
-            divided[u, qb] = work.tile([P, BR, DK], F32, name="divided", bufs=4)
+            nc.vector.reciprocal(recip[:], sums[p, qb][:, :, DK : DK + 1])
+            divided[p, qb] = work.tile([P, BR, DK], F32, name="divided", bufs=4)
             for br in range(BR):
                 nc.scalar.activation(
-                    divided[u, qb][:, br, :], sums[u, qb][:, br, 0:DK], ACT.Copy, scale=recip[:, br, :]
+                    divided[p, qb][:, br, :], sums[p, qb][:, br, 0:DK], ACT.Copy, scale=recip[:, br, :]
                 )
 
         att_ps_of = {}
 
-        def turn_and_add(u, qb):
+        def turn_and_add(p, qb):
             if qb == 0:
-                att_ps_of[u] = psum.tile([P, IC], F32, name="att_ps", bufs=1)
+                att_ps_of[p] = psum.tile([P, passes[p][2]], F32, name="att_ps", bufs=1)
             for br in range(BR):
                 nc.tensor.matmul(
-                    att_ps_of[u][:, qb * P : (qb + 1) * P],
-                    lhsT=divided[u, qb][:, br, :],
+                    att_ps_of[p][:, qb * P : (qb + 1) * P],
+                    lhsT=divided[p, qb][:, br, :],
                     rhs=ident_f32[:],
                     start=(br == 0),
                     stop=(br == BR - 1),
@@ -252,33 +261,40 @@ def tile_multiheadattention_b_kernel(
 
         att_of = {}
 
-        def round_att(u):
+        def round_att(p):
+            u, lo, width = passes[p]
             b, c, h = units[u]
             if h == 0:
                 att_of[b, c] = work.tile([P, H, IC], BF16, name="att")
-            nc.scalar.copy(att_of[b, c][:, h, :], att_ps_of[u][:])
+            nc.scalar.copy(att_of[b, c][:, h, lo : lo + width], att_ps_of[p][:])
 
-        def project_out(b, c):
-            first_node = b * T + c * IC
+        def project_out(p):
+            u, lo, width = passes[p]
+            b, c = units[u][0:2]
+            first_node = b * T + c * IC + lo
             for cb in range(CB):
-                y_ps = psum.tile([P, IC], F32, name="y_ps", tag="proj")
+                y_ps = psum.tile([P, width], F32, name="y_ps", tag="proj")
                 for h in range(H):
                     nc.tensor.matmul(
                         y_ps[:],
                         lhsT=weights["wo"][:, h, cb * P : (cb + 1) * P],
-                        rhs=att_of[b, c][:, h, :],
+                        rhs=att_of[b, c][:, h, lo : lo + width],
                         start=(h == 0),
                         stop=(h == H - 1),
                     )
-                nc.scalar.copy(y_sb[cb][:, first_node : first_node + IC], y_ps[:])
+                nc.scalar.copy(y_sb[cb][:, first_node : first_node + width], y_ps[:])
 
         window = []
 
         def turn_of(step, lag):
-            u, i = divmod(step - lag, KT)
-            return (u, i) if 0 <= u < len(units) else None
+            p, i = divmod(step - lag, KT)
+            return (p, i) if 0 <= p < len(passes) else None
 
-        for step in range(-PIECE_LEAD, KT * len(units) + OUT_LAG + 1):
+        def block_of(turn):
+            qb, rest = divmod(turn[1], BR)
+            return qb if rest == 0 and qb * P < passes[turn[0]][2] else None
+
+        for step in range(-PIECE_LEAD, KT * len(passes) + OUT_LAG + 1):
             for b in range(B):
                 for name, h, n, first_use in qk_pieces:
                     if step == b * STEPS_OF_GRAPH + first_use - PIECE_LEAD:
@@ -286,39 +302,43 @@ def tile_multiheadattention_b_kernel(
 
             now = turn_of(step, 0)
             if now:
-                u, kb = now
+                u, lo, width = passes[now[0]]
+                kb = now[1]
                 b, c, h = units[u]
-
-                if kb == 0 and u + 2 >= len(units):
+                unit_begins = kb == 0 and lo == 0
+                if unit_begins and u + 2 >= len(units):
                     cb = u + 2 - len(units)
                     window.append(work.tile([P, S], F32, name="window", tag="factor", bufs=3))
                     nc.sync.dma_start(window[cb][:], base[cb * P : (cb + 1) * P, :])
-                if kb == 0 and u == len(units) // B - 1:
+                if unit_begins and u == len(units) // B - 1:
                     for name, x_dram in (("k", k), ("q", q), ("v", v)):
                         load_nodes(nc.sync, name, x_dram, 1, 0, T)
-                if kb == 0 and u + 2 < len(units):
+                if unit_begins and u + 2 < len(units):
                     load_unit(u + 2, NEXT_BLOCKS if u == 0 else KT)
-                exponentials(u, kb)
+                exponentials(now[0], kb)
 
             summing = turn_of(step, SUM_LAG)
-            if summing:
+            if summing and summing[1] // BR * P < passes[summing[0]][2]:
                 weighted_sums(summing[0], summing[1] // BR, summing[1] % BR)
             dividing = turn_of(step, NORM_LAG)
-            if dividing and dividing[1] % BR == 0:
-                divide(dividing[0], dividing[1] // BR)
+            if dividing and block_of(dividing) is not None:
+                divide(dividing[0], block_of(dividing))
             turning = turn_of(step, FLIP_LAG)
-            if turning and turning[1] % BR == 0:
-                turn_and_add(turning[0], turning[1] // BR)
+            if turning and block_of(turning) is not None:
+                turn_and_add(turning[0], block_of(turning))
             rounding = turn_of(step, ATT_LAG)
             if rounding and rounding[1] == 0:
                 round_att(rounding[0])
             leaving = turn_of(step, OUT_LAG)
-            if leaving and leaving[1] == 0 and units[leaving[0]][2] == H - 1:
-                project_out(units[leaving[0]][0], units[leaving[0]][1])
+            if leaving and leaving[1] == 0 and units[passes[leaving[0]][0]][2] == H - 1:
+                project_out(leaving[0])
 
             masking = turn_of(step, -MASK_LEAD)
-            if masking:
-                mask_factors(masking[0], masking[1])
+            if masking and passes[masking[0]][1] == 0:
+                u_ahead = passes[masking[0]][0]
+                if u_ahead == 0:
+                    local_mask(nc.vector, 0, masking[1])
+                mask_factors(u_ahead, masking[1])
 
             if now:
                 v_piece = step - b * STEPS_OF_GRAPH - V_LAG

@@ -111,11 +111,12 @@ def tile_multiheadattention_b_kernel(
             queue.dma_start(bias_col[name][:], b_dram.rearrange("(a p) o -> p (a o)", p=P))
 
         load_weight(nc.scalar, "wk", wk)
-        load_nodes(nc.scalar, "k", k, 0, 0, T)
+        load_nodes(nc.scalar, "k", k, 0, 0, BANK)
         load_bias(nc.scalar, "bk", bk)
         load_weight(nc.scalar, "wq", wq)
         load_nodes(nc.scalar, "q", q, 0, 0, IC)
         load_bias(nc.scalar, "bq", bq)
+        load_nodes(nc.scalar, "k", k, 0, BANK, T - BANK)
         load_blocks(0, 0, FIRST_BLOCKS)
         load_bias(nc.sync, "bo", bo)
         load_blocks(0, FIRST_BLOCKS, FIRST_BLOCKS)
@@ -189,9 +190,11 @@ def tile_multiheadattention_b_kernel(
                 vh_ones[:, first : first + V_BLOCKS, :, 0:DK], v_ps[:].rearrange("p j (h d) -> p j h d", h=H)
             )
 
-        def mask_factors(u, kb):
+        def mask_factors(p, kb):
+            u, lo, width = passes[p]
             b, c, h = units[u]
-            nc.vector.tensor_tensor(factor[u][:, kb, :, :], factor[u][:, kb, :, :], mask_of[b, c][:, kb, :, :], ALU.mult)
+            part = factor[u][:, kb, :, lo : lo + width]
+            nc.vector.tensor_tensor(part, part, mask_of[b, c][:, kb, :, lo : lo + width], ALU.mult)
 
         expo = {}
 
@@ -201,7 +204,7 @@ def tile_multiheadattention_b_kernel(
             first_query = b * T + c * IC + lo
             if kb == 0:
                 expo[p] = work.tile([P, KT, BR, width], BF16, name="expo")
-            raw_ps = psum.tile([P, width], F32, name="raw_ps", bufs=3)
+            raw_ps = psum.tile([P, width], F32, name="raw_ps", bufs=2)
             nc.tensor.matmul(
                 raw_ps[:],
                 lhsT=kh[:, h, b * T + kb * P : b * T + (kb + 1) * P],
@@ -223,7 +226,7 @@ def tile_multiheadattention_b_kernel(
         def weighted_sums(p, qb, br):
             b, c, h = units[passes[p][0]]
             if br == 0:
-                sums[p, qb] = psum.tile([P, BR, BANK // BR], F32, name="sums_ps")
+                sums[p, qb] = psum.tile([P, BR, BANK // BR], F32, name="sums_ps", bufs=3)
             for kb in range(KT):
                 nc.tensor.matmul(
                     sums[p, qb][:, br, 0 : DK + 1],
@@ -334,11 +337,10 @@ def tile_multiheadattention_b_kernel(
                 project_out(leaving[0])
 
             masking = turn_of(step, -MASK_LEAD)
-            if masking and passes[masking[0]][1] == 0:
-                u_ahead = passes[masking[0]][0]
-                if u_ahead == 0:
+            if masking:
+                if masking[0] == 0:
                     local_mask(nc.vector, 0, masking[1])
-                mask_factors(u_ahead, masking[1])
+                mask_factors(masking[0], masking[1])
 
             if now:
                 v_piece = step - b * STEPS_OF_GRAPH - V_LAG

@@ -110,14 +110,14 @@ def tile_multiheadattention_b_kernel(
             bias_col[name] = held.tile([P, CB], F32, name=name + "_col")
             queue.dma_start(bias_col[name][:], b_dram.rearrange("(a p) o -> p (a o)", p=P))
 
-        load_weight(nc.scalar, "wk", wk)
-        load_nodes(nc.scalar, "k", k, 0, 0, BANK)
-        load_bias(nc.scalar, "bk", bk)
         load_weight(nc.scalar, "wq", wq)
         load_nodes(nc.scalar, "q", q, 0, 0, IC)
+        load_bias(nc.scalar, "bk", bk)
         load_bias(nc.scalar, "bq", bq)
-        load_nodes(nc.scalar, "k", k, 0, BANK, T - BANK)
+        load_weight(nc.sync, "wk", wk)
+        load_nodes(nc.sync, "k", k, 0, 0, BANK)
         load_blocks(0, 0, FIRST_BLOCKS)
+        load_nodes(nc.scalar, "k", k, 0, BANK, T - BANK)
         load_bias(nc.sync, "bo", bo)
         load_blocks(0, FIRST_BLOCKS, FIRST_BLOCKS)
         load_blocks(0, 2 * FIRST_BLOCKS, FIRST_BLOCKS)

from contextlib import ExitStack

import concourse.mybir as mybir
from concourse.masks import make_identity

BF16, F32, U16 = mybir.dt.bfloat16, mybir.dt.float32, mybir.dt.uint16
ALU = mybir.AluOpType
ACT = mybir.ActivationFunctionType

P = 128
B, T, C, H, DK, S, N = 2, 1024, 256, 2, 128, 4096, 2048
SCALE = 32.0**-0.5
BR = 2
CB = C // P
KT = T // P
BANK = 512
IC = BANK
QB = IC // P
CHUNKS = T // IC
VROW = DK + 2

SUM_LAG = KT
NORM_LAG = SUM_LAG + BR
FLIP_LAG = NORM_LAG + 2
ATT_LAG = FLIP_LAG + BR * (QB - 1) + 1
OUT_LAG = ATT_LAG + 1
STEPS_OF_GRAPH = CHUNKS * H * KT
V_BLOCKS = 2
V_PIECES = KT // V_BLOCKS
V_LAG = SUM_LAG - V_PIECES
FIRST_BLOCKS = 2
NEXT_BLOCKS = 4
PIECE_LEAD = 3
MASK_LEAD = 2

FLOPS = 4 * 2 * C * C * N + 3 * B * H * 2 * DK * T * T


def tile_multiheadattention_b_kernel(
    tc, q, k, v, adj, adj1, attn_bias, edge_bias, wq, bq, wk, bk, wv, bv, wo, bo, base, offs, out
):
    nc = tc.nc
    units = [(b, c, h) for b in range(B) for c in range(CHUNKS) for h in range(H)]
    passes = [(u, 0, IC) for u in range(len(units) - 1)]
    passes += [(len(units) - 1, 0, IC // 2), (len(units) - 1, IC // 2, IC // 2)]
    with ExitStack() as ctx:
        held = ctx.enter_context(tc.tile_pool(name="held", bufs=1))
        work = ctx.enter_context(tc.tile_pool(name="work", bufs=2))
        psum = ctx.enter_context(tc.psum_pool(name="psum", bufs=2))

        offsets = held.tile([P, N // 16], U16, name="offsets")

        staged = {}

        def load_nodes(queue, name, x_dram, b, first, count):
            if first == 0:
                staged[name, b] = work.tile([P, CB, T], BF16, name=name + "_sb", bufs=1)
            queue.dma_start(
                staged[name, b][:, :, first : first + count],
                x_dram[:, b * T + first : b * T + first + count].rearrange("(e p) n -> p e n", p=P),
            )

        mask_of = {}
        adj1_of = {}
        factor = {}

        def load_blocks(u, k0, blocks):
            b, c, h = units[u]
            lo = c * IC
            if k0 == 0 and h == 0:
                mask_of[b, c] = work.tile([P, KT, BR, IC], BF16, name="masks")
                adj1_of[b, c] = work.tile([P, KT, IC], BF16, name="adj1_sb")
            if k0 == 0:
                factor[u] = work.tile([P, KT, BR, IC], BF16, name="factor", bufs=3)
            keys = slice(k0 * P, (k0 + blocks) * P)
            pairs = [
                (factor[u][:, k0 : k0 + blocks, 0, :], attn_bias[b, h, keys, lo : lo + IC]),
                (factor[u][:, k0 : k0 + blocks, 1, :], edge_bias[b, h, keys, lo : lo + IC]),
            ]
            if h == 0:
                pairs = [
                    (mask_of[b, c][:, k0 : k0 + blocks, 0, :], adj[b, keys, lo : lo + IC]),
                    (adj1_of[b, c][:, k0 : k0 + blocks, :], adj1[b, keys, lo : lo + IC]),
                ] + pairs
            for tile_part, dram_part in pairs:
                nc.sync.dma_start(tile_part, dram_part.rearrange("(k p) i -> p k i", p=P))
            if h == 0 and u > 0:
                for kb in range(k0, k0 + blocks):
                    local_mask(nc.gpsimd, u, kb)

        def local_mask(engine, u, kb):
            b, c, h = units[u]
            engine.tensor_tensor(
                mask_of[b, c][:, kb, 1, :], mask_of[b, c][:, kb, 0, :], adj1_of[b, c][:, kb, :], ALU.mult
            )

        def load_unit(u, blocks):
            for k0 in range(0, KT, blocks):
                load_blocks(u, k0, blocks)

        weights = {}

        def load_weight(queue, name, w_dram):
            weights[name] = held.tile([P, CB, C], BF16, name=name)
            queue.dma_start(weights[name][:], w_dram.rearrange("(e p) c -> p e c", p=P))

        bias_col = {}

        def load_bias(queue, name, b_dram):
            bias_col[name] = held.tile([P, CB], F32, name=name + "_col")
            queue.dma_start(bias_col[name][:], b_dram.rearrange("(a p) o -> p (a o)", p=P))

        load_weight(nc.scalar, "wq", wq)
        load_nodes(nc.scalar, "q", q, 0, 0, IC)
        load_bias(nc.scalar, "bk", bk)
        load_bias(nc.scalar, "bq", bq)
        load_weight(nc.sync, "wk", wk)
        load_nodes(nc.sync, "k", k, 0, 0, BANK)
        load_blocks(0, 0, FIRST_BLOCKS)
        load_nodes(nc.scalar, "k", k, 0, BANK, T - BANK)
        load_bias(nc.sync, "bo", bo)
        load_blocks(0, FIRST_BLOCKS, FIRST_BLOCKS)
        load_blocks(0, 2 * FIRST_BLOCKS, FIRST_BLOCKS)
        load_weight(nc.sync, "wv", wv)
        load_nodes(nc.sync, "v", v, 0, 0, T)

        ident_f32 = held.tile([P, P], F32, name="ident_f32")
        make_identity(nc, ident_f32[:])
        ones_row = held.tile([P, P], F32, name="ones_row")
        nc.vector.memset(ones_row[:], 0.0)
        nc.vector.memset(ones_row[0:1, :], 1.0)
        bv_row = held.tile([P, C], F32, name="bv_row")
        nc.vector.memset(bv_row[:], 0.0)
        nc.sync.dma_start(bv_row[0:1, :], bv.rearrange("c o -> o c"))
        load_blocks(0, 3 * FIRST_BLOCKS, FIRST_BLOCKS)
        load_unit(1, NEXT_BLOCKS)
        load_nodes(nc.sync, "q", q, 0, IC, T - IC)
        load_weight(nc.sync, "wo", wo)
        nc.sync.dma_start(offsets[:], offs)

        qh = held.tile([P, H, N], BF16, name="qh")
        kh = held.tile([P, H, N], BF16, name="kh")
        vh_ones = held.tile([P, B * KT, H, VROW], BF16, name="vh_ones")
        nc.gpsimd.memset(vh_ones[:], 1.0)
        y_sb = [held.tile([P, N], F32, name=f"y_sb{cb}") for cb in range(CB)]
        bo_wide = [held.tile([P, N], F32, name=f"bo_wide{cb}") for cb in range(CB)]
        for cb in range(CB):
            nc.scalar.activation(bo_wide[cb][:], bias_col["bo"][:, cb : cb + 1].to_broadcast([P, N]), ACT.Copy)

        def project(dst, w_sb, x_sb, bias, h, n, by_vector):
            proj_ps = psum.tile([P, BANK], F32, name="proj_ps", tag="proj")
            for e in range(CB):
                nc.tensor.matmul(
                    proj_ps[:],
                    lhsT=w_sb[:, e, h * P : (h + 1) * P],
                    rhs=x_sb[:, e, n * BANK : (n + 1) * BANK],
                    start=(e == 0),
                    stop=(e == CB - 1),
                )
            if by_vector:
                nc.vector.tensor_scalar_add(dst, proj_ps[:], bias[:, h : h + 1])
            else:
                nc.scalar.activation(dst, proj_ps[:], ACT.Identity, bias=bias[:, h : h + 1])

        def project_qk(b, name, h, n, by_vector):
            dst = kh if name == "k" else qh
            project(
                dst[:, h, b * T + n * BANK : b * T + (n + 1) * BANK],
                weights["w" + name], staged[name, b], bias_col["b" + name], h, n, by_vector,
            )

        qk_pieces = [("k", h, n, h * KT + n * (BANK // P)) for h in range(H) for n in range(T // BANK)]
        qk_pieces += [("q", h, n, (n * H + h) * KT) for h in range(H) for n in range(T // BANK)]

        def project_v(b, piece):
            v_ps = psum.tile([P, V_BLOCKS, C], F32, name="v_ps", tag="proj")
            for j in range(V_BLOCKS):
                kb = piece * V_BLOCKS + j
                for e in range(CB):
                    nc.tensor.matmul(
                        v_ps[:, j, :],
                        lhsT=staged["v", b][:, e, kb * P : (kb + 1) * P],
                        rhs=weights["wv"][:, e, :],
                        start=(e == 0),
                        stop=False,
                    )
                nc.tensor.matmul(v_ps[:, j, :], lhsT=ones_row[:], rhs=bv_row[:], start=False, stop=True)
            first = b * KT + piece * V_BLOCKS
            nc.scalar.copy(
                vh_ones[:, first : first + V_BLOCKS, :, 0:DK], v_ps[:].rearrange("p j (h d) -> p j h d", h=H)
            )

        def mask_factors(p, kb):
            u, lo, width = passes[p]
            b, c, h = units[u]
            part = factor[u][:, kb, :, lo : lo + width]
            nc.vector.tensor_tensor(part, part, mask_of[b, c][:, kb, :, lo : lo + width], ALU.mult)

        expo = {}

        def exponentials(p, kb):
            u, lo, width = passes[p]
            b, c, h = units[u]
            first_query = b * T + c * IC + lo
            if kb == 0:
                expo[p] = work.tile([P, KT, BR, width], BF16, name="expo")
            raw_ps = psum.tile([P, width], F32, name="raw_ps", bufs=2)
            nc.tensor.matmul(
                raw_ps[:],
                lhsT=kh[:, h, b * T + kb * P : b * T + (kb + 1) * P],
                rhs=qh[:, h, first_query : first_query + width],
                start=True,
                stop=True,
            )
            logit = work.tile([P, BR, width], F32, name="logit", bufs=4)
            nc.vector.tensor_tensor(
                logit[:],
                raw_ps[:].unsqueeze(1).to_broadcast([P, BR, width]),
                factor[u][:, kb, :, lo : lo + width],
                ALU.mult,
            )
            nc.scalar.activation(expo[p][:, kb, :, :], logit[:], ACT.Exp, scale=SCALE)

        sums = {}

        def weighted_sums(p, qb, br):
            b, c, h = units[passes[p][0]]
            if br == 0:
                sums[p, qb] = psum.tile([P, BR, BANK // BR], F32, name="sums_ps", bufs=3)
            for kb in range(KT):
                nc.tensor.matmul(
                    sums[p, qb][:, br, 0 : DK + 1],
                    lhsT=expo[p][:, kb, br, qb * P : (qb + 1) * P],
                    rhs=vh_ones[:, b * KT + kb, h, 0 : DK + 1],
                    start=(kb == 0),
                    stop=(kb == KT - 1),
                )

        divided = {}

        def divide(p, qb):
            recip = work.tile([P, BR, 1], F32, name="recip", bufs=4)
            nc.vector.reciprocal(recip[:], sums[p, qb][:, :, DK : DK + 1])
            divided[p, qb] = work.tile([P, BR, DK], F32, name="divided", bufs=4)
            for br in range(BR):
                nc.scalar.activation(
                    divided[p, qb][:, br, :], sums[p, qb][:, br, 0:DK], ACT.Copy, scale=recip[:, br, :]
                )

        att_ps_of = {}

        def turn_and_add(p, qb):
            if qb == 0:
                att_ps_of[p] = psum.tile([P, passes[p][2]], F32, name="att_ps", bufs=1)
            for br in range(BR):
                nc.tensor.matmul(
                    att_ps_of[p][:, qb * P : (qb + 1) * P],
                    lhsT=divided[p, qb][:, br, :],
                    rhs=ident_f32[:],
                    start=(br == 0),
                    stop=(br == BR - 1),
                    is_transpose=True,
                )

        att_of = {}

        def round_att(p):
            u, lo, width = passes[p]
            b, c, h = units[u]
            if h == 0:
                att_of[b, c] = work.tile([P, H, IC], BF16, name="att")
            nc.scalar.copy(att_of[b, c][:, h, lo : lo + width], att_ps_of[p][:])

        def project_out(p):
            u, lo, width = passes[p]
            b, c = units[u][0:2]
            first_node = b * T + c * IC + lo
            for cb in range(CB):
                y_ps = psum.tile([P, width], F32, name="y_ps", tag="proj")
                for h in range(H):
                    nc.tensor.matmul(
                        y_ps[:],
                        lhsT=weights["wo"][:, h, cb * P : (cb + 1) * P],
                        rhs=att_of[b, c][:, h, lo : lo + width],
                        start=(h == 0),
                        stop=(h == H - 1),
                    )
                nc.scalar.copy(y_sb[cb][:, first_node : first_node + width], y_ps[:])

        window = []

        def turn_of(step, lag):
            p, i = divmod(step - lag, KT)
            return (p, i) if 0 <= p < len(passes) else None

        def block_of(turn):
            qb, rest = divmod(turn[1], BR)
            return qb if rest == 0 and qb * P < passes[turn[0]][2] else None

        for step in range(-PIECE_LEAD, KT * len(passes) + OUT_LAG + 1):
            for b in range(B):
                for name, h, n, first_use in qk_pieces:
                    if step == b * STEPS_OF_GRAPH + first_use - PIECE_LEAD:
                        project_qk(b, name, h, n, by_vector=step < 0)

            now = turn_of(step, 0)
            if now:
                u, lo, width = passes[now[0]]
                kb = now[1]
                b, c, h = units[u]
                unit_begins = kb == 0 and lo == 0
                if unit_begins and u + 2 >= len(units):
                    cb = u + 2 - len(units)
                    window.append(work.tile([P, S], F32, name="window", tag="factor", bufs=3))
                    nc.sync.dma_start(window[cb][:], base[cb * P : (cb + 1) * P, :])
                if unit_begins and u == len(units) // B - 1:
                    for name, x_dram in (("k", k), ("q", q), ("v", v)):
                        load_nodes(nc.sync, name, x_dram, 1, 0, T)
                if unit_begins and u + 2 < len(units):
                    load_unit(u + 2, NEXT_BLOCKS if u == 0 else KT)
                exponentials(now[0], kb)

            summing = turn_of(step, SUM_LAG)
            if summing and summing[1] // BR * P < passes[summing[0]][2]:
                weighted_sums(summing[0], summing[1] // BR, summing[1] % BR)
            dividing = turn_of(step, NORM_LAG)
            if dividing and block_of(dividing) is not None:
                divide(dividing[0], block_of(dividing))
            turning = turn_of(step, FLIP_LAG)
            if turning and block_of(turning) is not None:
                turn_and_add(turning[0], block_of(turning))
            rounding = turn_of(step, ATT_LAG)
            if rounding and rounding[1] == 0:
                round_att(rounding[0])
            leaving = turn_of(step, OUT_LAG)
            if leaving and leaving[1] == 0 and units[passes[leaving[0]][0]][2] == H - 1:
                project_out(leaving[0])

            masking = turn_of(step, -MASK_LEAD)
            if masking:
                if masking[0] == 0:
                    local_mask(nc.vector, 0, masking[1])
                mask_factors(masking[0], masking[1])

            if now:
                v_piece = step - b * STEPS_OF_GRAPH - V_LAG
                if 0 <= v_piece < V_PIECES:
                    project_v(b, v_piece)

        for cb in range(CB):
            nc.vector.tensor_tensor(window[cb][:].indirect(offsets[:]), y_sb[cb][:], bo_wide[cb][:], ALU.add)
            nc.sync.dma_start(out[cb * P : (cb + 1) * P, :], window[cb][:])
